import numpy as np
import ml_dtypes


def mxq(x, axis, fmt="e4m3"):
    dtype, down = {"e4m3": (ml_dtypes.float8_e4m3fn, 7), "e5m2": (ml_dtypes.float8_e5m2, 14)}[fmt]
    v = np.moveaxis(np.asarray(x, np.float32).astype(ml_dtypes.bfloat16).astype(np.float64), axis, -1)
    blocks = v.reshape(v.shape[:-1] + (-1, 32))
    amax = np.abs(blocks).max(-1, keepdims=True)
    byte = np.maximum(np.where(amax > 0, np.frexp(amax)[1] - 1 + 127, 0) - down, 1)
    scale = np.exp2(byte - 127.0)
    codes = (blocks / scale).astype(np.float32).astype(dtype).astype(np.float64)
    return np.moveaxis((codes * scale).reshape(v.shape), -1, axis)


WIDE = False


def mx_kscale(k):
    if not WIDE:
        return np.ones(k)
    levels = np.array([10, -10, 5, -5, 0])
    if k % 512:
        return np.exp2(np.random.permutation(np.resize(levels, k // 32))).repeat(32)
    a = np.empty((k // 512, 16))
    for p in range(k // 512):
        a[p, :8] = np.random.permutation(np.resize(levels, 8))
        for g in range(8):
            far = levels[np.abs(levels - a[p, g]) >= 10]
            a[p, g + 8] = far[np.random.randint(len(far))]
    return np.exp2(a.ravel()).repeat(32)


BF16 = ml_dtypes.bfloat16


def bf(x):
    return np.asarray(x, np.float32).astype(BF16)


def f64(x):
    return np.asarray(x).astype(np.float64)


B, L, D, H, HD, MINI, NCH, TEXT, OFF = 4, 1024, 512, 8, 64, 64, 4, 64, 128


def rope_table():
    inv_freq = 1.0 / (10000.0 ** (np.arange(0, HD, 2) / HD))
    ang = np.outer(np.arange(L), inv_freq)
    return np.stack([np.cos(ang), np.sin(ang)], axis=-1)


def l2norm(x):
    return x / np.maximum(np.sqrt((x * x).sum(-1, keepdims=True)), 1e-12)


def rope(x, cos, sin):
    c = cos[None, :, None, :]
    s = sin[None, :, None, :]
    xr, xi = x[..., 0::2], x[..., 1::2]
    return np.stack([xr * c - xi * s, xr * s + xi * c], axis=-1).reshape(x.shape)


def draw0():
    s = mx_kscale(D)
    return {"hidden_states": bf(np.random.standard_normal((B, L, D)) * s),
            "freqs_cis": bf(rope_table()),
            "wq_w": bf(np.random.standard_normal((D, D)) / np.sqrt(D) / s[:, None]),
            "wq_b": bf(np.random.standard_normal(D) * 0.1),
            "wu_w": bf(np.random.standard_normal((D, D)) / np.sqrt(D) / s[:, None]),
            "wu_b": bf(np.random.standard_normal(D) * 0.1)}


def core(hidden_states, freqs_cis, wq_w, wq_b, wu_w, wu_b):
    hq = mxq(f64(hidden_states), 2, "e4m3")
    xq = ((hq @ mxq(f64(wq_w), 0, "e4m3")) + f64(wq_b)).reshape(B, L, H, HD)
    xu = ((hq @ mxq(f64(wu_w), 0, "e4m3")) + f64(wu_b)).reshape(B, L, H, HD)
    fc = f64(freqs_cis)
    cos, sin = fc[..., 0], fc[..., 1]
    return rope(l2norm(xq), cos, sin), rope(l2norm(xu), cos, sin)


def e4m3fn_bytes(y):
    return np.clip(np.asarray(y, np.float64), -448.0, 448.0).astype(np.float32).astype(ml_dtypes.float8_e4m3fn).view(np.uint8)


def e4m3fn_values(b):
    return np.asarray(b, np.uint8).view(ml_dtypes.float8_e4m3fn).astype(np.float64)


def setup_inputs():
    d = draw0()
    x0 = np.asarray(d['hidden_states']).astype(np.float64)
    s = (np.max(np.abs(x0), axis=(0, 1), keepdims=True) / 448.0).astype(np.float32)
    out = {}
    for k, v in d.items():
        if k == 'hidden_states':
            out['hidden_states_bytes'] = e4m3fn_bytes(x0 / s.astype(np.float64))
            out['hidden_states_scale'] = s
        else:
            out[k] = v
    return out


def reference(hidden_states_bytes, hidden_states_scale, freqs_cis, wq_w, wq_b, wu_w, wu_b):
    return core(e4m3fn_values(hidden_states_bytes) * hidden_states_scale.astype(np.float64), freqs_cis, wq_w, wq_b, wu_w, wu_b)

@@ -1,0 +1,399 @@
+from contextlib import ExitStack
+
+import concourse.mybir as mybir
+from concourse.masks import make_identity
+
+FLOPS = 2 * 4096 * 512 * 1024
+
+F32 = mybir.dt.float32
+BF16 = mybir.dt.bfloat16
+U32 = mybir.dt.uint32
+U8 = mybir.dt.uint8
+FP8 = mybir.dt.float8_e4m3fn
+FP8X4 = mybir.dt.float8_e4m3fn_x4
+ALU = mybir.AluOpType
+ACT = mybir.ActivationFunctionType
+AX = mybir.AxisListType
+
+P = 128
+NG = 8
+NSTEP = 32
+TAIL_FROM = 30
+V_EVERY = 1000
+
+
+def tile_tttwrapper_pb_t_kernel(
+    tc, hidden_states_bytes, hidden_states_scale, freqs_cis, wq_w, wq_b, wu_w, wu_b, out_0, out_1
+):
+    nc = tc.nc
+    with ExitStack() as ctx:
+        const = ctx.enter_context(tc.tile_pool(name="const", bufs=1))
+        setup = ctx.enter_context(tc.tile_pool(name="setup", bufs=1))
+        work = ctx.enter_context(tc.tile_pool(name="work", bufs=2))
+        ps_xt = ctx.enter_context(tc.psum_pool(name="ps_xt", bufs=1))
+        ps_mx = ctx.enter_context(tc.psum_pool(name="ps_mx", bufs=4))
+        ps_bt = ctx.enter_context(tc.psum_pool(name="ps_bt", bufs=2))
+        ps_ss = ctx.enter_context(tc.psum_pool(name="ps_ss", bufs=1))
+
+        hid = hidden_states_bytes.rearrange("b l k -> (b l) k")
+        outs = [
+            out_0.rearrange("b l h d -> (b l) (h d)"),
+            out_1.rearrange("b l h d -> (b l) (h d)"),
+        ]
+
+        hb = []
+        for g in range(NG):
+            hb_g = const.tile([P, 2048], U8, name="hbytes%d" % g, tag="hbytes%d" % g)
+            hb.append(hb_g)
+        nc.sync.dma_start(
+            out=hb[0][:], in_=hid[0:512, :].rearrange("(p i) k -> p (i k)", i=4)
+        )
+        sc = const.tile([P, 512], F32, name="sc", tag="sc")
+        nc.scalar.dma_start(
+            out=sc[:], in_=hidden_states_scale.rearrange("a b k -> (a b k)").partition_broadcast(P)
+        )
+        wraw = []
+        for s, w in enumerate((wq_w, wu_w)):
+            wr = setup.tile([P, 4, 512], BF16, name="wraw%d" % s, tag="wraw%d" % s)
+            nc.sync.dma_start(out=wr[:], in_=w.rearrange("(p t) n -> p t n", t=4))
+            wraw.append(wr)
+        fr = setup.tile([P, 512], BF16, name="fr", tag="fr")
+        nc.scalar.dma_start(
+            out=fr[:].rearrange("p (hf x) -> p hf x", hf=2),
+            in_=freqs_cis.rearrange("(hf p i) j t -> p hf (i j t)", hf=2, p=P, i=4),
+        )
+        braw = setup.tile([P, 256], BF16, name="braw", tag="braw")
+        nc.vector.memset(braw[:], 0.0)
+        nc.scalar.dma_start(out=braw[0:2, :], in_=wq_b.rearrange("(r x) -> r x", r=2))
+        nc.scalar.dma_start(out=braw[2:4, :], in_=wu_b.rearrange("(r x) -> r x", r=2))
+        for g in range(1, NG):
+            nc.sync.dma_start(
+                out=hb[g][:],
+                in_=hid[g * 512 : (g + 1) * 512, :].rearrange("(p i) k -> p (i k)", i=4),
+            )
+
+        ident_f = const.tile([P, P], F32, name="ident_f", tag="ident_f")
+        make_identity(nc, ident_f[:])
+        ident_b = const.tile([P, P], BF16, name="ident_b", tag="ident_b")
+        make_identity(nc, ident_b[:])
+        ind = const.tile([P, 32], F32, name="ind", tag="ind")
+        nc.vector.memset(ind[:], 0.0)
+        nc.vector.tensor_reduce(
+            out=ind[:, 0:4],
+            in_=ident_f[:].rearrange("p (h j) -> p h j", h=4),
+            axis=AX.X,
+            op=ALU.add,
+        )
+        one = setup.tile([P, 1], F32, name="one", tag="one")
+        nc.vector.memset(one[:], 1.0)
+        junk = setup.tile([P, 1], F32, name="junk", tag="junk")
+        nc.scalar.activation(out=junk[:], in_=one[:], func=ACT.Sqrt)
+
+        wc = []
+        ws = []
+        wgs = []
+
+        def interleave_w(s, e, eng):
+            dst = wgs[s][:].rearrange("p (hq e x t) -> p hq e x t", hq=2, e=2, t=4)[:, :, e]
+            src = wraw[s][:].rearrange("p t (hq x e) -> p hq e x t", hq=2, e=2)[:, :, e]
+            if eng == "v":
+                nc.vector.tensor_copy(out=dst, in_=src)
+            elif eng == "s":
+                nc.scalar.copy(out=dst, in_=src)
+            else:
+                for hq in range(2):
+                    nc.gpsimd.tensor_scalar(
+                        out=dst[:, hq],
+                        in0=src[:, hq],
+                        scalar1=1.0,
+                        scalar2=0.0,
+                        op0=ALU.mult,
+                        op1=ALU.add,
+                    )
+
+        def quant_w(s):
+            wc_s = const.tile([P, 512], U32, name="wc%d" % s, tag="wc%d" % s, align_bytes=64)
+            ws_s = const.tile([P, 512], U8, name="ws%d" % s, tag="ws%d" % s, align_bytes=64)
+            nc.vector.quantize_mx(out=wc_s[:].bitcast(FP8X4), scales=ws_s[:], in_=wgs[s][:])
+            wc.append(wc_s)
+            ws.append(ws_s)
+
+        for s in range(2):
+            wg = setup.tile([P, 2048], BF16, name="wg%d" % s, tag="wg%d" % s, align_bytes=64)
+            wgs.append(wg)
+
+        xb = {}
+        xg = {}
+        hc = {}
+        hs = {}
+
+        def h1(g, i):
+            if i == 0:
+                xb_g = work.tile([P, 2048], BF16, name="xb", tag="xb")
+                xb[g] = xb_g
+            nc.vector.tensor_tensor(
+                out=xb[g][:, i * 512 : (i + 1) * 512],
+                in0=hb[g][:, i * 512 : (i + 1) * 512].bitcast(FP8),
+                in1=sc[:],
+                op=ALU.mult,
+            )
+
+        xts = {}
+
+        def h2(g, ip):
+            words = xb[g][:].bitcast(F32)
+            xt = ps_xt.tile([P, 512], F32, name="xt", tag="xt")
+            for i2 in range(2):
+                i = ip * 2 + i2
+                for u in range(2):
+                    nc.tensor.transpose(
+                        xt[:, (i2 * 2 + u) * P : (i2 * 2 + u + 1) * P],
+                        words[:, i * 256 + u : (i + 1) * 256 : 2],
+                        ident_f[:],
+                    )
+            xts[(g, ip)] = xt
+
+        def h3(g, ip):
+            if ip == 0:
+                xg_g = work.tile([P, 2048], BF16, name="xg", tag="xg", align_bytes=64)
+                xg[g] = xg_g
+            nc.scalar.copy(
+                out=xg[g][:].bitcast(F32)[:, ip * 512 : (ip + 1) * 512].rearrange(
+                    "p (i r u) -> p i r u", i=2, u=2
+                ),
+                in_=xts[(g, ip)][:].rearrange("p (i u r) -> p i r u", i=2, u=2),
+            )
+
+        def h4(g):
+            hc_g = work.tile([P, 512], U32, name="hc", tag="hc", align_bytes=64)
+            hs_g = work.tile([P, 512], U8, name="hs", tag="hs", align_bytes=64)
+            nc.vector.quantize_mx(out=hc_g[:].bitcast(FP8X4), scales=hs_g[:], in_=xg[g][:])
+            hc[g] = hc_g
+            hs[g] = hs_g
+
+        exs = []
+        for k in range(2):
+            ex = setup.tile([P, 1024], BF16, name="ex%d" % k, tag="ex%d" % k)
+            src = (
+                fr[:]
+                .rearrange("p (a j k) -> p a j k", a=8, k=2)[:, :, :, k]
+                .unsqueeze(2)
+                .to_broadcast([P, 8, 4, 32])
+            )
+            dst = ex[:].rearrange("p (a h j) -> p a h j", a=8, h=4)
+            if k == 0:
+                nc.vector.tensor_copy(out=dst, in_=src)
+            else:
+                nc.scalar.copy(out=dst, in_=src)
+            exs.append(ex)
+        interleave_w(0, 0, "v")
+        interleave_w(0, 1, "s")
+        interleave_w(1, 0, "g")
+        interleave_w(1, 1, "g")
+        quant_w(0)
+        h1(0, 0)
+        h1(0, 1)
+        h2(0, 0)
+        h3(0, 0)
+        h1(0, 2)
+        h1(0, 3)
+        h2(0, 1)
+        h3(0, 1)
+        h4(0)
+
+        tabs = []
+        for k in range(2):
+            tp = ps_bt.tile([P, 1024], BF16, name="tp", tag="bt")
+            for a in range(8):
+                nc.tensor.transpose(
+                    tp[:, a * P : (a + 1) * P], exs[k][:, a * P : (a + 1) * P], ident_b[:]
+                )
+            tab = const.tile([P, 1024], BF16, name="tab%d" % k, tag="tab%d" % k)
+            nc.scalar.copy(out=tab[:], in_=tp[:])
+            tabs.append(tab)
+
+        bde = setup.tile([P, 256], BF16, name="bde", tag="bde")
+        nc.vector.tensor_copy(
+            out=bde[:].rearrange("p (e x) -> p e x", e=2),
+            in_=braw[:].rearrange("p (x e) -> p e x", e=2),
+        )
+        bp = ps_ss.tile([P, 256], BF16, name="bp", tag="ssp")
+        for e in range(2):
+            nc.tensor.transpose(bp[:, e * P : (e + 1) * P], bde[:, e * P : (e + 1) * P], ident_b[:])
+        bcol = const.tile([P, 8], F32, name="bcol", tag="bcol")
+        nc.vector.tensor_copy(
+            out=bcol[:].rearrange("p (e r) -> p e r", e=2),
+            in_=bp[:].rearrange("p (e r) -> p e r", e=2)[:, :, 0:4],
+        )
+        quant_w(1)
+
+        acc = {}
+        sq = {}
+        rot = {}
+        rn = {}
+        bts = {}
+        ssps = {}
+
+        def bias_col(t, e):
+            st = t % 4
+            return bcol[:, e * 4 + st : e * 4 + st + 1]
+
+        def mx(t):
+            g, st = divmod(t, 4)
+            s, hq = divmod(st, 2)
+            pair = []
+            for e in range(2):
+                a = ps_mx.tile([P, 512], F32, name="acc", tag="acc")
+                c0 = hq * 256 + e * P
+                nc.tensor.matmul_mx(
+                    out=a[:],
+                    lhsT=wc[s][:, c0 : c0 + P].bitcast(FP8X4),
+                    lhsT_scale=ws[s][:, c0 : c0 + P],
+                    rhs=hc[g][:].bitcast(FP8X4),
+                    rhs_scale=hs[g][:],
+                    start=True,
+                    stop=True,
+                )
+                pair.append(a)
+            acc[t] = pair
+
+        def products(t):
+            hf = (t // 4) % 2
+            cs = [tabs[k][:, hf * 512 : (hf + 1) * 512] for k in range(2)]
+            a = acc[t]
+            add_eng = nc.vector if t >= TAIL_FROM else nc.gpsimd
+
+            def prod(e, k, nm):
+                pt = work.tile([P, 512], F32, name=nm, tag=nm)
+                nc.vector.scalar_tensor_tensor(
+                    out=pt[:], in0=a[e][:], scalar=bias_col(t, e), in1=cs[k], op0=ALU.add, op1=ALU.mult
+                )
+                return pt
+
+            p1 = prod(0, 0, "p1")
+            p3 = prod(0, 1, "p3")
+            p2 = prod(1, 1, "p2")
+            o0 = work.tile([P, 512], F32, name="o0", tag="o0", bufs=4)
+            add_eng.tensor_tensor(out=o0[:], in0=p1[:], in1=p2[:], op=ALU.subtract)
+            p4 = prod(1, 0, "p4")
+            o1 = work.tile([P, 512], F32, name="o1", tag="o1", bufs=4)
+            add_eng.tensor_tensor(out=o1[:], in0=p3[:], in1=p4[:], op=ALU.add)
+            rot[t] = (o0, o1)
+
+        def squares(t):
+            qs = []
+            for e in range(2):
+                qt = work.tile([P, 512], F32, name="sq%d" % e, tag="sq%d" % e, bufs=2)
+                nc.scalar.activation(
+                    out=qt[:], in_=acc[t][e][:], func=ACT.Square, bias=bias_col(t, e), scale=1.0
+                )
+                qs.append(qt)
+            sq[t] = qs
+
+        def sumsq(t):
+            ssp = ps_ss.tile([P, 128], F32, name="ssp", tag="ssp")
+            for i in range(4):
+                for e in range(2):
+                    nc.tensor.matmul(
+                        out=ssp[:, i * 32 : (i + 1) * 32],
+                        lhsT=sq[t][e][:, i * P : (i + 1) * P],
+                        rhs=ind[:],
+                        start=(e == 0),
+                        stop=(e == 1),
+                    )
+            ssps[t] = ssp
+
+        def rchain_v(t):
+            t1 = work.tile([P, 16], F32, name="t1", tag="t1")
+            nc.vector.tensor_scalar(
+                out=t1[:].rearrange("p (i h) -> p i h", i=4),
+                in0=ssps[t][:].rearrange("p (i n) -> p i n", i=4)[:, :, 0:4],
+                scalar1=1e-24,
+                scalar2=None,
+                op0=ALU.max,
+            )
+            t2 = work.tile([P, 16], F32, name="t2", tag="t2")
+            nc.vector.reciprocal(out=t2[:], in_=t1[:])
+            rn[t] = t2
+
+        def rchain_s(t):
+            r = work.tile([P, 16], F32, name="r", tag="r", bufs=3)
+            nc.scalar.activation(out=r[:], in_=rn[t][:], func=ACT.Sqrt)
+            rn[t] = r
+
+        def back(t):
+            banks = []
+            for ip in range(2):
+                bt = ps_bt.tile([P, 512], F32, name="bt", tag="bt")
+                for e in range(2):
+                    for i2 in range(2):
+                        i = ip * 2 + i2
+                        nc.tensor.transpose(
+                            bt[:, e * 256 + i2 * P : e * 256 + (i2 + 1) * P],
+                            rot[t][e][:, i * P : (i + 1) * P],
+                            ident_f[:],
+                        )
+                banks.append(bt)
+            bts[t] = banks
+
+        def evac(t):
+            g, st = divmod(t, 4)
+            s, hq = divmod(st, 2)
+            r = rn[t]
+            ot = work.tile([P, 4, 256], F32, name="ot", tag="ot", bufs=3)
+            for ip in range(2):
+                v = bts[t][ip][:].rearrange("p (e i h j) -> p e i h j", e=2, i=2, h=4)
+                for i2 in range(2):
+                    i = ip * 2 + i2
+                    if ip == 1 and (t >= TAIL_FROM or t % V_EVERY == V_EVERY - 1):
+                        nc.vector.tensor_tensor(
+                            out=ot[:, i, :].rearrange("p (h j e) -> p h j e", h=4, e=2),
+                            in0=v[:, :, i2].rearrange("p e h j -> p h j e"),
+                            in1=r[:, i * 4 : (i + 1) * 4]
+                            .unsqueeze(2)
+                            .unsqueeze(3)
+                            .to_broadcast([P, 4, 32, 2]),
+                            op=ALU.mult,
+                        )
+                    else:
+                        for h in range(4):
+                            nc.scalar.activation(
+                                out=ot[:, i, h * 64 : (h + 1) * 64].rearrange("p (j e) -> p j e", e=2),
+                                in_=v[:, :, i2, h, :].rearrange("p e j -> p j e"),
+                                func=ACT.Copy,
+                                scale=r[:, i * 4 + h : i * 4 + h + 1],
+                            )
+            nc.sync.dma_start(
+                out=outs[s][g * 512 : (g + 1) * 512, hq * 256 : (hq + 1) * 256].rearrange(
+                    "(p i) c -> p i c", i=4
+                ),
+                in_=ot[:],
+            )
+
+        mx(0)
+        for t in range(NSTEP + 2):
+            g, st = divmod(t, 4)
+            nxt = g + 1
+            more = t < NSTEP and nxt < NG
+            if t >= 2:
+                rchain_v(t - 2)
+                back(t - 2)
+            if 1 <= t <= NSTEP:
+                squares(t - 1)
+            if more and st in (1, 2):
+                h2(nxt, st - 1)
+                h3(nxt, st - 1)
+            if 1 <= t <= NSTEP:
+                sumsq(t - 1)
+            if t + 1 < NSTEP:
+                mx(t + 1)
+            if t < NSTEP:
+                products(t)
+            if t >= 2:
+                rchain_s(t - 2)
+                evac(t - 2)
+            if more and st == 2:
+                h4(nxt)
+            if more and st in (0, 1):
+                h1(nxt, 2 * st)
+                h1(nxt, 2 * st + 1)

@@ -48,9 +48,12 @@ def tile_tttwrapper_pb_t_kernel(
         nc.sync.dma_start(
             out=hb[0][:], in_=hid[0:512, :].rearrange("(p i) k -> p (i k)", i=4)
         )
-        sc = const.tile([P, 512], F32, name="sc", tag="sc")
+        sc = const.tile([P, 1024], F32, name="sc", tag="sc")
         nc.scalar.dma_start(
-            out=sc[:], in_=hidden_states_scale.rearrange("a b k -> (a b k)").partition_broadcast(P)
+            out=sc[:, 0:512], in_=hidden_states_scale.rearrange("a b k -> (a b k)").partition_broadcast(P)
+        )
+        nc.gpsimd.tensor_scalar(
+            out=sc[:, 512:1024], in0=sc[:, 0:512], scalar1=1.0, scalar2=0.0, op0=ALU.mult, op1=ALU.add
         )
         wraw = []
         for s, w in enumerate((wq_w, wu_w)):
@@ -87,7 +90,7 @@ def tile_tttwrapper_pb_t_kernel(
         one = setup.tile([P, 1], F32, name="one", tag="one")
         nc.vector.memset(one[:], 1.0)
         junk = setup.tile([P, 1], F32, name="junk", tag="junk")
-        nc.scalar.activation(out=junk[:], in_=one[:], func=ACT.Sqrt)
+        nc.scalar.activation(out=junk[:], in_=one[:], func=ACT.Abs_reciprocal_sqrt)
 
         wc = []
         ws = []
@@ -134,6 +137,17 @@ def tile_tttwrapper_pb_t_kernel(
             nc.vector.tensor_tensor(
                 out=xb[g][:, i * 512 : (i + 1) * 512],
                 in0=hb[g][:, i * 512 : (i + 1) * 512].bitcast(FP8),
+                in1=sc[:, 0:512],
+                op=ALU.mult,
+            )
+
+        def h1w(g, ip):
+            if ip == 0:
+                xb_g = work.tile([P, 2048], BF16, name="xb", tag="xb")
+                xb[g] = xb_g
+            nc.vector.tensor_tensor(
+                out=xb[g][:, ip * 1024 : (ip + 1) * 1024],
+                in0=hb[g][:, ip * 1024 : (ip + 1) * 1024].bitcast(FP8),
                 in1=sc[:],
                 op=ALU.mult,
             )
@@ -271,10 +285,16 @@ def tile_tttwrapper_pb_t_kernel(
                 return pt
 
             p1 = prod(0, 0, "p1")
-            p3 = prod(0, 1, "p3")
+            g, st = divmod(t, 4)
+            if g + 1 < NG:
+                if st in (0, 1):
+                    h1w(g + 1, st)
+                elif st == 2:
+                    h4(g + 1)
             p2 = prod(1, 1, "p2")
             o0 = work.tile([P, 512], F32, name="o0", tag="o0", bufs=4)
             add_eng.tensor_tensor(out=o0[:], in0=p1[:], in1=p2[:], op=ALU.subtract)
+            p3 = prod(0, 1, "p3")
             p4 = prod(1, 0, "p4")
             o1 = work.tile([P, 512], F32, name="o1", tag="o1", bufs=4)
             add_eng.tensor_tensor(out=o1[:], in0=p3[:], in1=p4[:], op=ALU.add)
@@ -312,13 +332,11 @@ def tile_tttwrapper_pb_t_kernel(
                 scalar2=None,
                 op0=ALU.max,
             )
-            t2 = work.tile([P, 16], F32, name="t2", tag="t2")
-            nc.vector.reciprocal(out=t2[:], in_=t1[:])
-            rn[t] = t2
+            rn[t] = t1
 
         def rchain_s(t):
             r = work.tile([P, 16], F32, name="r", tag="r", bufs=3)
-            nc.scalar.activation(out=r[:], in_=rn[t][:], func=ACT.Sqrt)
+            nc.scalar.activation(out=r[:], in_=rn[t][:], func=ACT.Abs_reciprocal_sqrt)
             rn[t] = r
 
         def back(t):
@@ -371,6 +389,7 @@ def tile_tttwrapper_pb_t_kernel(
             )
 
         mx(0)
+        ctx.enter_context(tc.manual_schedule(engines={mybir.EngineType.DVE}))
         for t in range(NSTEP + 2):
             g, st = divmod(t, 4)
             nxt = g + 1
@@ -380,20 +399,15 @@ def tile_tttwrapper_pb_t_kernel(
                 back(t - 2)
             if 1 <= t <= NSTEP:
                 squares(t - 1)
-            if more and st in (1, 2):
-                h2(nxt, st - 1)
-                h3(nxt, st - 1)
             if 1 <= t <= NSTEP:
                 sumsq(t - 1)
             if t + 1 < NSTEP:
                 mx(t + 1)
             if t < NSTEP:
                 products(t)
+            if more and st in (0, 1):
+                h2(nxt, st)
+                h3(nxt, st)
             if t >= 2:
                 rchain_s(t - 2)
                 evac(t - 2)
-            if more and st == 2:
-                h4(nxt)
-            if more and st in (0, 1):
-                h1(nxt, 2 * st)
-                h1(nxt, 2 * st + 1)

@@ -89,6 +89,9 @@ def tile_tttwrapper_pb_t_kernel(
         )
         one = setup.tile([P, 1], F32, name="one", tag="one")
         nc.vector.memset(one[:], 1.0)
+        eps = const.tile([P, 2], F32, name="eps", tag="eps")
+        nc.vector.memset(eps[:, 0:1], -1e-24)
+        nc.vector.memset(eps[:, 1:2], 1e-24)
         junk = setup.tile([P, 1], F32, name="junk", tag="junk")
         nc.scalar.activation(out=junk[:], in_=one[:], func=ACT.Abs_reciprocal_sqrt)
 
@@ -285,12 +288,6 @@ def tile_tttwrapper_pb_t_kernel(
                 return pt
 
             p1 = prod(0, 0, "p1")
-            g, st = divmod(t, 4)
-            if g + 1 < NG:
-                if st in (0, 1):
-                    h1w(g + 1, st)
-                elif st == 2:
-                    h4(g + 1)
             p2 = prod(1, 1, "p2")
             o0 = work.tile([P, 512], F32, name="o0", tag="o0", bufs=4)
             add_eng.tensor_tensor(out=o0[:], in0=p1[:], in1=p2[:], op=ALU.subtract)
@@ -323,44 +320,45 @@ def tile_tttwrapper_pb_t_kernel(
                     )
             ssps[t] = ssp
 
-        def rchain_v(t):
+        def norm(t):
             t1 = work.tile([P, 16], F32, name="t1", tag="t1")
-            nc.vector.tensor_scalar(
+            nc.scalar.activation(
                 out=t1[:].rearrange("p (i h) -> p i h", i=4),
-                in0=ssps[t][:].rearrange("p (i n) -> p i n", i=4)[:, :, 0:4],
-                scalar1=1e-24,
-                scalar2=None,
-                op0=ALU.max,
+                in_=ssps[t][:].rearrange("p (i n) -> p i n", i=4)[:, :, 0:4],
+                func=ACT.Relu,
+                bias=eps[:, 0:1],
+                scale=1.0,
             )
-            rn[t] = t1
-
-        def rchain_s(t):
             r = work.tile([P, 16], F32, name="r", tag="r", bufs=3)
-            nc.scalar.activation(out=r[:], in_=rn[t][:], func=ACT.Abs_reciprocal_sqrt)
+            nc.scalar.activation(
+                out=r[:], in_=t1[:], func=ACT.Abs_reciprocal_sqrt, bias=eps[:, 1:2], scale=1.0
+            )
             rn[t] = r
 
-        def back(t):
-            banks = []
-            for ip in range(2):
-                bt = ps_bt.tile([P, 512], F32, name="bt", tag="bt")
-                for e in range(2):
-                    for i2 in range(2):
-                        i = ip * 2 + i2
-                        nc.tensor.transpose(
-                            bt[:, e * 256 + i2 * P : e * 256 + (i2 + 1) * P],
-                            rot[t][e][:, i * P : (i + 1) * P],
-                            ident_f[:],
-                        )
-                banks.append(bt)
-            bts[t] = banks
+        def back(t, ip):
+            bt = ps_bt.tile([P, 512], F32, name="bt", tag="bt")
+            for e in range(2):
+                for i2 in range(2):
+                    i = ip * 2 + i2
+                    nc.tensor.transpose(
+                        bt[:, e * 256 + i2 * P : e * 256 + (i2 + 1) * P],
+                        rot[t][e][:, i * P : (i + 1) * P],
+                        ident_f[:],
+                    )
+            bts[(t, ip)] = bt
 
-        def evac(t):
+        ots = {}
+
+        def evac(t, ip):
             g, st = divmod(t, 4)
             s, hq = divmod(st, 2)
             r = rn[t]
-            ot = work.tile([P, 4, 256], F32, name="ot", tag="ot", bufs=3)
-            for ip in range(2):
-                v = bts[t][ip][:].rearrange("p (e i h j) -> p e i h j", e=2, i=2, h=4)
+            if ip == 0:
+                ot_t = work.tile([P, 4, 256], F32, name="ot", tag="ot", bufs=3)
+                ots[t] = ot_t
+            ot = ots[t]
+            if True:
+                v = bts[(t, ip)][:].rearrange("p (e i h j) -> p e i h j", e=2, i=2, h=4)
                 for i2 in range(2):
                     i = ip * 2 + i2
                     if ip == 1 and (t >= TAIL_FROM or t % V_EVERY == V_EVERY - 1):
@@ -381,33 +379,42 @@ def tile_tttwrapper_pb_t_kernel(
                                 func=ACT.Copy,
                                 scale=r[:, i * 4 + h : i * 4 + h + 1],
                             )
-            nc.sync.dma_start(
-                out=outs[s][g * 512 : (g + 1) * 512, hq * 256 : (hq + 1) * 256].rearrange(
-                    "(p i) c -> p i c", i=4
-                ),
-                in_=ot[:],
-            )
+            if ip == 1:
+                nc.sync.dma_start(
+                    out=outs[s][g * 512 : (g + 1) * 512, hq * 256 : (hq + 1) * 256].rearrange(
+                        "(p i) c -> p i c", i=4
+                    ),
+                    in_=ot[:],
+                )
 
         mx(0)
-        ctx.enter_context(tc.manual_schedule(engines={mybir.EngineType.DVE}))
+        ctx.enter_context(tc.manual_schedule())
         for t in range(NSTEP + 2):
             g, st = divmod(t, 4)
             nxt = g + 1
             more = t < NSTEP and nxt < NG
             if t >= 2:
-                rchain_v(t - 2)
-                back(t - 2)
+                back(t - 2, 0)
             if 1 <= t <= NSTEP:
                 squares(t - 1)
-            if 1 <= t <= NSTEP:
-                sumsq(t - 1)
+            if t >= 2:
+                norm(t - 2)
+            if more and st in (1, 2):
+                h2(nxt, st - 1)
+            if t >= 2:
+                evac(t - 2, 0)
+                back(t - 2, 1)
+            if more and st in (1, 2):
+                h3(nxt, st - 1)
+            if more and st in (0, 1):
+                h1w(nxt, st)
             if t + 1 < NSTEP:
                 mx(t + 1)
+            if t >= 2:
+                evac(t - 2, 1)
             if t < NSTEP:
                 products(t)
-            if more and st in (0, 1):
-                h2(nxt, st)
-                h3(nxt, st)
-            if t >= 2:
-                rchain_s(t - 2)
-                evac(t - 2)
+            if more and st == 2:
+                h4(nxt)
+            if 1 <= t <= NSTEP:
+                sumsq(t - 1)

@@ -19,7 +19,6 @@ P = 128
 NG = 8
 NSTEP = 32
 TAIL_FROM = 30
-V_EVERY = 1000
 
 
 def tile_tttwrapper_pb_t_kernel(
@@ -79,14 +78,6 @@ def tile_tttwrapper_pb_t_kernel(
         make_identity(nc, ident_f[:])
         ident_b = const.tile([P, P], BF16, name="ident_b", tag="ident_b")
         make_identity(nc, ident_b[:])
-        ind = const.tile([P, 32], F32, name="ind", tag="ind")
-        nc.vector.memset(ind[:], 0.0)
-        nc.vector.tensor_reduce(
-            out=ind[:, 0:4],
-            in_=ident_f[:].rearrange("p (h j) -> p h j", h=4),
-            axis=AX.X,
-            op=ALU.add,
-        )
         one = setup.tile([P, 1], F32, name="one", tag="one")
         nc.vector.memset(one[:], 1.0)
         eps = const.tile([P, 2], F32, name="eps", tag="eps")
@@ -250,6 +241,7 @@ def tile_tttwrapper_pb_t_kernel(
         rn = {}
         bts = {}
         ssps = {}
+        sss = {}
 
         def bias_col(t, e):
             st = t % 4
@@ -274,7 +266,7 @@ def tile_tttwrapper_pb_t_kernel(
                 pair.append(a)
             acc[t] = pair
 
-        def products(t):
+        def products(t, mid):
             hf = (t // 4) % 2
             cs = [tabs[k][:, hf * 512 : (hf + 1) * 512] for k in range(2)]
             a = acc[t]
@@ -291,6 +283,7 @@ def tile_tttwrapper_pb_t_kernel(
             p2 = prod(1, 1, "p2")
             o0 = work.tile([P, 512], F32, name="o0", tag="o0", bufs=4)
             add_eng.tensor_tensor(out=o0[:], in0=p1[:], in1=p2[:], op=ALU.subtract)
+            mid()
             p3 = prod(0, 1, "p3")
             p4 = prod(1, 0, "p4")
             o1 = work.tile([P, 512], F32, name="o1", tag="o1", bufs=4)
@@ -308,23 +301,34 @@ def tile_tttwrapper_pb_t_kernel(
             sq[t] = qs
 
         def sumsq(t):
-            ssp = ps_ss.tile([P, 128], F32, name="ssp", tag="ssp")
+            ssp = ps_ss.tile([P, 512], F32, name="ssp", tag="ssp")
             for i in range(4):
                 for e in range(2):
                     nc.tensor.matmul(
-                        out=ssp[:, i * 32 : (i + 1) * 32],
+                        out=ssp[:, i * P : (i + 1) * P],
                         lhsT=sq[t][e][:, i * P : (i + 1) * P],
-                        rhs=ind[:],
+                        rhs=ident_f[:],
+                        is_transpose=True,
                         start=(e == 0),
                         stop=(e == 1),
                     )
             ssps[t] = ssp
 
+        def reduce(t):
+            ss = work.tile([P, 16], F32, name="ss", tag="ss", bufs=3)
+            nc.vector.tensor_reduce(
+                out=ss[:],
+                in_=ssps[t][:].rearrange("p (i h j) -> p (i h) j", i=4, h=4),
+                axis=AX.X,
+                op=ALU.add,
+            )
+            sss[t] = ss
+
         def norm(t):
             t1 = work.tile([P, 16], F32, name="t1", tag="t1")
             nc.scalar.activation(
-                out=t1[:].rearrange("p (i h) -> p i h", i=4),
-                in_=ssps[t][:].rearrange("p (i n) -> p i n", i=4)[:, :, 0:4],
+                out=t1[:],
+                in_=sss[t][:],
                 func=ACT.Relu,
                 bias=eps[:, 0:1],
                 scale=1.0,
@@ -336,7 +340,10 @@ def tile_tttwrapper_pb_t_kernel(
             rn[t] = r
 
         def back(t, ip):
-            bt = ps_bt.tile([P, 512], F32, name="bt", tag="bt")
+            if t >= NSTEP - 2:
+                bt = ps_mx.tile([P, 512], F32, name="acc", tag="acc")
+            else:
+                bt = ps_bt.tile([P, 512], F32, name="bt", tag="bt")
             for e in range(2):
                 for i2 in range(2):
                     i = ip * 2 + i2
@@ -357,28 +364,24 @@ def tile_tttwrapper_pb_t_kernel(
                 ot_t = work.tile([P, 4, 256], F32, name="ot", tag="ot", bufs=3)
                 ots[t] = ot_t
             ot = ots[t]
-            if True:
+            if ip == 1 and t >= TAIL_FROM:
+                nc.vector.tensor_tensor(
+                    out=ot[:, 2:4, :].rearrange("p i (h j e) -> p (i h) j e", h=4, e=2),
+                    in0=bts[(t, ip)][:].rearrange("p (e i h j) -> p (i h) j e", e=2, i=2, h=4),
+                    in1=r[:, 8:16].unsqueeze(2).unsqueeze(3).to_broadcast([P, 8, 32, 2]),
+                    op=ALU.mult,
+                )
+            else:
                 v = bts[(t, ip)][:].rearrange("p (e i h j) -> p e i h j", e=2, i=2, h=4)
                 for i2 in range(2):
                     i = ip * 2 + i2
-                    if ip == 1 and (t >= TAIL_FROM or t % V_EVERY == V_EVERY - 1):
-                        nc.vector.tensor_tensor(
-                            out=ot[:, i, :].rearrange("p (h j e) -> p h j e", h=4, e=2),
-                            in0=v[:, :, i2].rearrange("p e h j -> p h j e"),
-                            in1=r[:, i * 4 : (i + 1) * 4]
-                            .unsqueeze(2)
-                            .unsqueeze(3)
-                            .to_broadcast([P, 4, 32, 2]),
-                            op=ALU.mult,
+                    for h in range(4):
+                        nc.scalar.activation(
+                            out=ot[:, i, h * 64 : (h + 1) * 64].rearrange("p (j e) -> p j e", e=2),
+                            in_=v[:, :, i2, h, :].rearrange("p e j -> p j e"),
+                            func=ACT.Copy,
+                            scale=r[:, i * 4 + h : i * 4 + h + 1],
                         )
-                    else:
-                        for h in range(4):
-                            nc.scalar.activation(
-                                out=ot[:, i, h * 64 : (h + 1) * 64].rearrange("p (j e) -> p j e", e=2),
-                                in_=v[:, :, i2, h, :].rearrange("p e j -> p j e"),
-                                func=ACT.Copy,
-                                scale=r[:, i * 4 + h : i * 4 + h + 1],
-                            )
             if ip == 1:
                 nc.sync.dma_start(
                     out=outs[s][g * 512 : (g + 1) * 512, hq * 256 : (hq + 1) * 256].rearrange(
@@ -389,32 +392,52 @@ def tile_tttwrapper_pb_t_kernel(
 
         mx(0)
         ctx.enter_context(tc.manual_schedule())
-        for t in range(NSTEP + 2):
+        for t in range(NSTEP):
             g, st = divmod(t, 4)
             nxt = g + 1
-            more = t < NSTEP and nxt < NG
-            if t >= 2:
-                back(t - 2, 0)
-            if 1 <= t <= NSTEP:
+            more = nxt < NG
+            if t >= 3:
+                back(t - 3, 0)
+            if t >= 1:
                 squares(t - 1)
-            if t >= 2:
-                norm(t - 2)
             if more and st in (1, 2):
                 h2(nxt, st - 1)
-            if t >= 2:
-                evac(t - 2, 0)
-                back(t - 2, 1)
+            if t >= 3:
+                evac(t - 3, 0)
+                back(t - 3, 1)
             if more and st in (1, 2):
                 h3(nxt, st - 1)
             if more and st in (0, 1):
                 h1w(nxt, st)
             if t + 1 < NSTEP:
                 mx(t + 1)
+            if t >= 3:
+                evac(t - 3, 1)
             if t >= 2:
-                evac(t - 2, 1)
-            if t < NSTEP:
-                products(t)
+                products(t, lambda: reduce(t - 2))
+                norm(t - 2)
+            else:
+                products(t, lambda: None)
             if more and st == 2:
                 h4(nxt)
-            if 1 <= t <= NSTEP:
+            if t >= 1:
                 sumsq(t - 1)
+        last = NSTEP - 1
+        squares(last)
+        reduce(last - 1)
+        norm(last - 1)
+        back(last - 2, 0)
+        back(last - 2, 1)
+        back(last - 1, 0)
+        back(last - 1, 1)
+        sumsq(last)
+        evac(last - 2, 0)
+        evac(last - 2, 1)
+        reduce(last)
+        back(last, 0)
+        back(last, 1)
+        evac(last - 1, 0)
+        evac(last - 1, 1)
+        norm(last)
+        evac(last, 0)
+        evac(last, 1)

@@ -219,6 +219,9 @@ def tile_tttwrapper_pb_t_kernel(
             tab = const.tile([P, 1024], BF16, name="tab%d" % k, tag="tab%d" % k)
             nc.scalar.copy(out=tab[:], in_=tp[:])
             tabs.append(tab)
+        neg = const.tile([P, 1024], BF16, name="tab2", tag="tab2")
+        nc.scalar.mul(out=neg[:], in_=tp[:], mul=-1.0)
+        tabs.append(neg)
 
         bde = setup.tile([P, 256], BF16, name="bde", tag="bde")
         nc.vector.tensor_copy(
@@ -268,27 +271,24 @@ def tile_tttwrapper_pb_t_kernel(
 
         def products(t, mid):
             hf = (t // 4) % 2
-            cs = [tabs[k][:, hf * 512 : (hf + 1) * 512] for k in range(2)]
-            a = acc[t]
+            cs = [tab_k[:, hf * 512 : (hf + 1) * 512] for tab_k in tabs]
             add_eng = nc.vector if t >= TAIL_FROM else nc.gpsimd
+            pa = work.tile([P, 1024], F32, name="pa", tag="pa", bufs=3)
+            pb = work.tile([P, 1024], F32, name="pb", tag="pb", bufs=3)
 
-            def prod(e, k, nm):
-                pt = work.tile([P, 512], F32, name=nm, tag=nm)
+            def prod(out, e, k):
                 nc.vector.scalar_tensor_tensor(
-                    out=pt[:], in0=a[e][:], scalar=bias_col(t, e), in1=cs[k], op0=ALU.add, op1=ALU.mult
+                    out=out, in0=acc[t][e][:], scalar=bias_col(t, e), in1=cs[k], op0=ALU.add, op1=ALU.mult
                 )
-                return pt
 
-            p1 = prod(0, 0, "p1")
-            p2 = prod(1, 1, "p2")
-            o0 = work.tile([P, 512], F32, name="o0", tag="o0", bufs=4)
-            add_eng.tensor_tensor(out=o0[:], in0=p1[:], in1=p2[:], op=ALU.subtract)
+            prod(pa[:, 0:512], 0, 0)
+            prod(pb[:, 0:512], 1, 2)
             mid()
-            p3 = prod(0, 1, "p3")
-            p4 = prod(1, 0, "p4")
-            o1 = work.tile([P, 512], F32, name="o1", tag="o1", bufs=4)
-            add_eng.tensor_tensor(out=o1[:], in0=p3[:], in1=p4[:], op=ALU.add)
-            rot[t] = (o0, o1)
+            prod(pa[:, 512:1024], 0, 1)
+            prod(pb[:, 512:1024], 1, 0)
+            o = work.tile([P, 1024], F32, name="o", tag="o", bufs=4)
+            add_eng.tensor_tensor(out=o[:], in0=pa[:], in1=pb[:], op=ALU.add)
+            rot[t] = o
 
         def squares(t):
             qs = []
@@ -349,7 +349,7 @@ def tile_tttwrapper_pb_t_kernel(
                     i = ip * 2 + i2
                     nc.tensor.transpose(
                         bt[:, e * 256 + i2 * P : e * 256 + (i2 + 1) * P],
-                        rot[t][e][:, i * P : (i + 1) * P],
+                        rot[t][:, e * 512 + i * P : e * 512 + (i + 1) * P],
                         ident_f[:],
                     )
             bts[(t, ip)] = bt

@@ -40,6 +40,8 @@ def tile_tttwrapper_pb_t_kernel(
             out_1.rearrange("b l h d -> (b l) (h d)"),
         ]
 
+        ctx.enter_context(tc.manual_schedule())
+
         hb = []
         for g in range(NG):
             hb_g = const.tile([P, 2048], U8, name="hbytes%d" % g, tag="hbytes%d" % g)
@@ -51,9 +53,6 @@ def tile_tttwrapper_pb_t_kernel(
         nc.scalar.dma_start(
             out=sc[:, 0:512], in_=hidden_states_scale.rearrange("a b k -> (a b k)").partition_broadcast(P)
         )
-        nc.gpsimd.tensor_scalar(
-            out=sc[:, 512:1024], in0=sc[:, 0:512], scalar1=1.0, scalar2=0.0, op0=ALU.mult, op1=ALU.add
-        )
         wraw = []
         for s, w in enumerate((wq_w, wu_w)):
             wr = setup.tile([P, 4, 512], BF16, name="wraw%d" % s, tag="wraw%d" % s)
@@ -64,10 +63,13 @@ def tile_tttwrapper_pb_t_kernel(
             out=fr[:].rearrange("p (hf x) -> p hf x", hf=2),
             in_=freqs_cis.rearrange("(hf p i) j t -> p hf (i j t)", hf=2, p=P, i=4),
         )
-        braw = setup.tile([P, 256], BF16, name="braw", tag="braw")
-        nc.vector.memset(braw[:], 0.0)
-        nc.scalar.dma_start(out=braw[0:2, :], in_=wq_b.rearrange("(r x) -> r x", r=2))
-        nc.scalar.dma_start(out=braw[2:4, :], in_=wu_b.rearrange("(r x) -> r x", r=2))
+        braw = []
+        for s, b in enumerate((wq_b, wu_b)):
+            br = setup.tile([P, 4], BF16, name="braw%d" % s, tag="braw%d" % s)
+            nc.scalar.dma_start(
+                out=br[:].rearrange("p (q e) -> p q e", q=2), in_=b.rearrange("(q p e) -> p q e", q=2, e=2)
+            )
+            braw.append(br)
         for g in range(1, NG):
             nc.sync.dma_start(
                 out=hb[g][:],
@@ -89,35 +91,29 @@ def tile_tttwrapper_pb_t_kernel(
         wc = []
         ws = []
         wgs = []
-
-        def interleave_w(s, e, eng):
-            dst = wgs[s][:].rearrange("p (hq e x t) -> p hq e x t", hq=2, e=2, t=4)[:, :, e]
-            src = wraw[s][:].rearrange("p t (hq x e) -> p hq e x t", hq=2, e=2)[:, :, e]
-            if eng == "v":
-                nc.vector.tensor_copy(out=dst, in_=src)
-            elif eng == "s":
-                nc.scalar.copy(out=dst, in_=src)
-            else:
-                for hq in range(2):
-                    nc.gpsimd.tensor_scalar(
-                        out=dst[:, hq],
-                        in0=src[:, hq],
-                        scalar1=1.0,
-                        scalar2=0.0,
-                        op0=ALU.mult,
-                        op1=ALU.add,
-                    )
-
-        def quant_w(s):
-            wc_s = const.tile([P, 512], U32, name="wc%d" % s, tag="wc%d" % s, align_bytes=64)
-            ws_s = const.tile([P, 512], U8, name="ws%d" % s, tag="ws%d" % s, align_bytes=64)
-            nc.vector.quantize_mx(out=wc_s[:].bitcast(FP8X4), scales=ws_s[:], in_=wgs[s][:])
-            wc.append(wc_s)
-            ws.append(ws_s)
-
         for s in range(2):
             wg = setup.tile([P, 2048], BF16, name="wg%d" % s, tag="wg%d" % s, align_bytes=64)
             wgs.append(wg)
+            wc_s = const.tile([P, 512], U32, name="wc%d" % s, tag="wc%d" % s, align_bytes=64)
+            ws_s = const.tile([P, 512], U8, name="ws%d" % s, tag="ws%d" % s, align_bytes=64)
+            wc.append(wc_s)
+            ws.append(ws_s)
+
+        def interleave_w(s, hq, eng):
+            dst = wgs[s][:, hq * 1024 : (hq + 1) * 1024].rearrange("p (e x t) -> p e x t", e=2, t=4)
+            src = wraw[s][:, :, hq * 256 : (hq + 1) * 256].rearrange("p t (x e) -> p e x t", e=2)
+            if eng == "v":
+                nc.vector.tensor_copy(out=dst, in_=src)
+            else:
+                nc.scalar.copy(out=dst, in_=src)
+
+        def quant_w(s, hq):
+            cols = slice(hq * 256, (hq + 1) * 256)
+            nc.vector.quantize_mx(
+                out=wc[s][:, cols].bitcast(FP8X4),
+                scales=ws[s][:, cols],
+                in_=wgs[s][:, hq * 1024 : (hq + 1) * 1024],
+            )
 
         xb = {}
         xg = {}
@@ -150,7 +146,10 @@ def tile_tttwrapper_pb_t_kernel(
 
         def h2(g, ip):
             words = xb[g][:].bitcast(F32)
-            xt = ps_xt.tile([P, 512], F32, name="xt", tag="xt")
+            if g == 0 and ip == 1:
+                xt = ps_ss.tile([P, 512], F32, name="xt0", tag="ssp")
+            else:
+                xt = ps_xt.tile([P, 512], F32, name="xt", tag="xt")
             for i2 in range(2):
                 i = ip * 2 + i2
                 for u in range(2):
@@ -179,64 +178,68 @@ def tile_tttwrapper_pb_t_kernel(
             hc[g] = hc_g
             hs[g] = hs_g
 
-        exs = []
-        for k in range(2):
-            ex = setup.tile([P, 1024], BF16, name="ex%d" % k, tag="ex%d" % k)
-            src = (
-                fr[:]
-                .rearrange("p (a j k) -> p a j k", a=8, k=2)[:, :, :, k]
-                .unsqueeze(2)
-                .to_broadcast([P, 8, 4, 32])
+        exs = {}
+        tabs = {}
+
+        def spread(hf, k):
+            ex = setup.tile([P, 512], BF16, name="ex%d%d" % (hf, k), tag="ex%d%d" % (hf, k))
+            src = fr[:, hf * 256 : (hf + 1) * 256].rearrange("p (i j k) -> p i j k", i=4, k=2)[:, :, :, k]
+            nc.scalar.copy(
+                out=ex[:].rearrange("p (i h j) -> p i h j", i=4, h=4),
+                in_=src.unsqueeze(2).to_broadcast([P, 4, 4, 32]),
             )
-            dst = ex[:].rearrange("p (a h j) -> p a h j", a=8, h=4)
-            if k == 0:
-                nc.vector.tensor_copy(out=dst, in_=src)
-            else:
-                nc.scalar.copy(out=dst, in_=src)
-            exs.append(ex)
-        interleave_w(0, 0, "v")
-        interleave_w(0, 1, "s")
-        interleave_w(1, 0, "g")
-        interleave_w(1, 1, "g")
-        quant_w(0)
+            exs[(hf, k)] = ex
+
+        tps = {}
+
+        def turn(hf):
+            tp = ps_bt.tile([P, 1024], BF16, name="tp", tag="bt")
+            for k in range(2):
+                for i in range(4):
+                    nc.tensor.transpose(
+                        tp[:, k * 512 + i * P : k * 512 + (i + 1) * P],
+                        exs[(hf, k)][:, i * P : (i + 1) * P],
+                        ident_b[:],
+                    )
+            tps[hf] = tp
+
+        def table(hf):
+            tabs[hf] = []
+            for k in range(3):
+                tab = const.tile([P, 512], BF16, name="tab%d%d" % (hf, k), tag="tab%d%d" % (hf, k))
+                src = tps[hf][:, min(k, 1) * 512 : (min(k, 1) + 1) * 512]
+                if k < 2:
+                    nc.scalar.copy(out=tab[:], in_=src)
+                else:
+                    nc.scalar.mul(out=tab[:], in_=src, mul=-1.0)
+                tabs[hf].append(tab)
+
+        bcol = const.tile([P, 8], F32, name="bcol", tag="bcol")
+        nc.scalar.copy(out=sc[:, 512:1024], in_=sc[:, 0:512])
+        spread(0, 0)
+        spread(0, 1)
         h1(0, 0)
         h1(0, 1)
         h2(0, 0)
-        h3(0, 0)
         h1(0, 2)
         h1(0, 3)
+        h3(0, 0)
         h2(0, 1)
+        interleave_w(0, 0, "v")
+        interleave_w(0, 1, "v")
         h3(0, 1)
+        quant_w(0, 0)
+        for s in range(2):
+            nc.vector.tensor_copy(
+                out=bcol[:].rearrange("p (e u q) -> p u e q", e=2, u=2)[:, s],
+                in_=braw[s][:].rearrange("p (q e) -> p e q", q=2),
+            )
         h4(0)
-
-        tabs = []
-        for k in range(2):
-            tp = ps_bt.tile([P, 1024], BF16, name="tp", tag="bt")
-            for a in range(8):
-                nc.tensor.transpose(
-                    tp[:, a * P : (a + 1) * P], exs[k][:, a * P : (a + 1) * P], ident_b[:]
-                )
-            tab = const.tile([P, 1024], BF16, name="tab%d" % k, tag="tab%d" % k)
-            nc.scalar.copy(out=tab[:], in_=tp[:])
-            tabs.append(tab)
-        neg = const.tile([P, 1024], BF16, name="tab2", tag="tab2")
-        nc.scalar.mul(out=neg[:], in_=tp[:], mul=-1.0)
-        tabs.append(neg)
-
-        bde = setup.tile([P, 256], BF16, name="bde", tag="bde")
-        nc.vector.tensor_copy(
-            out=bde[:].rearrange("p (e x) -> p e x", e=2),
-            in_=braw[:].rearrange("p (x e) -> p e x", e=2),
-        )
-        bp = ps_ss.tile([P, 256], BF16, name="bp", tag="ssp")
-        for e in range(2):
-            nc.tensor.transpose(bp[:, e * P : (e + 1) * P], bde[:, e * P : (e + 1) * P], ident_b[:])
-        bcol = const.tile([P, 8], F32, name="bcol", tag="bcol")
-        nc.vector.tensor_copy(
-            out=bcol[:].rearrange("p (e r) -> p e r", e=2),
-            in_=bp[:].rearrange("p (e r) -> p e r", e=2)[:, :, 0:4],
-        )
-        quant_w(1)
+        quant_w(0, 1)
+        turn(0)
+        table(0)
+        interleave_w(1, 0, "s")
+        interleave_w(1, 1, "s")
 
         acc = {}
         sq = {}
@@ -245,6 +248,7 @@ def tile_tttwrapper_pb_t_kernel(
         bts = {}
         ssps = {}
         sss = {}
+        t1s = {}
 
         def bias_col(t, e):
             st = t % 4
@@ -270,15 +274,13 @@ def tile_tttwrapper_pb_t_kernel(
             acc[t] = pair
 
         def products(t, mid):
-            hf = (t // 4) % 2
-            cs = [tab_k[:, hf * 512 : (hf + 1) * 512] for tab_k in tabs]
-            add_eng = nc.vector if t >= TAIL_FROM else nc.gpsimd
+            cs = tabs[(t // 4) % 2]
             pa = work.tile([P, 1024], F32, name="pa", tag="pa", bufs=3)
             pb = work.tile([P, 1024], F32, name="pb", tag="pb", bufs=3)
 
             def prod(out, e, k):
                 nc.vector.scalar_tensor_tensor(
-                    out=out, in0=acc[t][e][:], scalar=bias_col(t, e), in1=cs[k], op0=ALU.add, op1=ALU.mult
+                    out=out, in0=acc[t][e][:], scalar=bias_col(t, e), in1=cs[k][:], op0=ALU.add, op1=ALU.mult
                 )
 
             prod(pa[:, 0:512], 0, 0)
@@ -286,19 +288,19 @@ def tile_tttwrapper_pb_t_kernel(
             mid()
             prod(pa[:, 512:1024], 0, 1)
             prod(pb[:, 512:1024], 1, 0)
-            o = work.tile([P, 1024], F32, name="o", tag="o", bufs=4)
-            add_eng.tensor_tensor(out=o[:], in0=pa[:], in1=pb[:], op=ALU.add)
-            rot[t] = o
+            if t < TAIL_FROM:
+                o = work.tile([P, 1024], F32, name="o", tag="o", bufs=4)
+                nc.gpsimd.tensor_tensor(out=o[:], in0=pa[:], in1=pb[:], op=ALU.add)
+                rot[t] = (o,)
+            else:
+                rot[t] = (pa, pb)
 
-        def squares(t):
-            qs = []
-            for e in range(2):
-                qt = work.tile([P, 512], F32, name="sq%d" % e, tag="sq%d" % e, bufs=2)
-                nc.scalar.activation(
-                    out=qt[:], in_=acc[t][e][:], func=ACT.Square, bias=bias_col(t, e), scale=1.0
-                )
-                qs.append(qt)
-            sq[t] = qs
+        def square(t, e):
+            qt = work.tile([P, 512], F32, name="sq%d" % e, tag="sq%d" % e, bufs=2)
+            nc.scalar.activation(
+                out=qt[:], in_=acc[t][e][:], func=ACT.Square, bias=bias_col(t, e), scale=1.0
+            )
+            sq[(t, e)] = qt
 
         def sumsq(t):
             ssp = ps_ss.tile([P, 512], F32, name="ssp", tag="ssp")
@@ -306,7 +308,7 @@ def tile_tttwrapper_pb_t_kernel(
                 for e in range(2):
                     nc.tensor.matmul(
                         out=ssp[:, i * P : (i + 1) * P],
-                        lhsT=sq[t][e][:, i * P : (i + 1) * P],
+                        lhsT=sq[(t, e)][:, i * P : (i + 1) * P],
                         rhs=ident_f[:],
                         is_transpose=True,
                         start=(e == 0),
@@ -324,8 +326,8 @@ def tile_tttwrapper_pb_t_kernel(
             )
             sss[t] = ss
 
-        def norm(t):
-            t1 = work.tile([P, 16], F32, name="t1", tag="t1")
+        def norm_a(t):
+            t1 = work.tile([P, 16], F32, name="t1", tag="t1", bufs=3)
             nc.scalar.activation(
                 out=t1[:],
                 in_=sss[t][:],
@@ -333,9 +335,12 @@ def tile_tttwrapper_pb_t_kernel(
                 bias=eps[:, 0:1],
                 scale=1.0,
             )
+            t1s[t] = t1
+
+        def norm_b(t):
             r = work.tile([P, 16], F32, name="r", tag="r", bufs=3)
             nc.scalar.activation(
-                out=r[:], in_=t1[:], func=ACT.Abs_reciprocal_sqrt, bias=eps[:, 1:2], scale=1.0
+                out=r[:], in_=t1s[t][:], func=ACT.Abs_reciprocal_sqrt, bias=eps[:, 1:2], scale=1.0
             )
             rn[t] = r
 
@@ -347,11 +352,16 @@ def tile_tttwrapper_pb_t_kernel(
             for e in range(2):
                 for i2 in range(2):
                     i = ip * 2 + i2
-                    nc.tensor.transpose(
-                        bt[:, e * 256 + i2 * P : e * 256 + (i2 + 1) * P],
-                        rot[t][:, e * 512 + i * P : e * 512 + (i + 1) * P],
-                        ident_f[:],
-                    )
+                    terms = rot[t]
+                    for n in range(len(terms)):
+                        nc.tensor.matmul(
+                            out=bt[:, e * 256 + i2 * P : e * 256 + (i2 + 1) * P],
+                            lhsT=terms[n][:, e * 512 + i * P : e * 512 + (i + 1) * P],
+                            rhs=ident_f[:],
+                            is_transpose=True,
+                            start=(n == 0),
+                            stop=(n == len(terms) - 1),
+                        )
             bts[(t, ip)] = bt
 
         ots = {}
@@ -360,11 +370,11 @@ def tile_tttwrapper_pb_t_kernel(
             g, st = divmod(t, 4)
             s, hq = divmod(st, 2)
             r = rn[t]
-            if ip == 0:
+            if t not in ots:
                 ot_t = work.tile([P, 4, 256], F32, name="ot", tag="ot", bufs=3)
                 ots[t] = ot_t
             ot = ots[t]
-            if ip == 1 and t >= TAIL_FROM:
+            if ip == 1 and t >= TAIL_FROM - 2:
                 nc.vector.tensor_tensor(
                     out=ot[:, 2:4, :].rearrange("p i (h j e) -> p (i h) j e", h=4, e=2),
                     in0=bts[(t, ip)][:].rearrange("p (e i h j) -> p (i h) j e", e=2, i=2, h=4),
@@ -382,16 +392,13 @@ def tile_tttwrapper_pb_t_kernel(
                             func=ACT.Copy,
                             scale=r[:, i * 4 + h : i * 4 + h + 1],
                         )
-            if ip == 1:
-                nc.sync.dma_start(
-                    out=outs[s][g * 512 : (g + 1) * 512, hq * 256 : (hq + 1) * 256].rearrange(
-                        "(p i) c -> p i c", i=4
-                    ),
-                    in_=ot[:],
-                )
+            outv = outs[s][g * 512 : (g + 1) * 512, hq * 256 : (hq + 1) * 256].rearrange("(p i) c -> p i c", i=4)
+            if t >= TAIL_FROM:
+                nc.sync.dma_start(out=outv[:, 2 * ip : 2 * ip + 2, :], in_=ot[:, 2 * ip : 2 * ip + 2, :])
+            elif ip == 1:
+                nc.sync.dma_start(out=outv, in_=ot[:])
 
         mx(0)
-        ctx.enter_context(tc.manual_schedule())
         for t in range(NSTEP):
             g, st = divmod(t, 4)
             nxt = g + 1
@@ -399,7 +406,11 @@ def tile_tttwrapper_pb_t_kernel(
             if t >= 3:
                 back(t - 3, 0)
             if t >= 1:
-                squares(t - 1)
+                square(t - 1, 0)
+            if t >= 3:
+                norm_b(t - 3)
+            if t >= 1:
+                square(t - 1, 1)
             if more and st in (1, 2):
                 h2(nxt, st - 1)
             if t >= 3:
@@ -407,37 +418,55 @@ def tile_tttwrapper_pb_t_kernel(
                 back(t - 3, 1)
             if more and st in (1, 2):
                 h3(nxt, st - 1)
-            if more and st in (0, 1):
+            if more and st in (0, 1) and t > 0:
                 h1w(nxt, st)
             if t + 1 < NSTEP:
                 mx(t + 1)
-            if t >= 3:
+            if t >= 3 and t < TAIL_FROM + 1:
                 evac(t - 3, 1)
-            if t >= 2:
-                products(t, lambda: reduce(t - 2))
-                norm(t - 2)
-            else:
-                products(t, lambda: None)
+
+            def mid():
+                if t >= 2:
+                    reduce(t - 2)
+                    norm_a(t - 2)
+
+            products(t, mid)
+            if t >= TAIL_FROM + 1:
+                evac(t - 3, 1)
             if more and st == 2:
                 h4(nxt)
             if t >= 1:
                 sumsq(t - 1)
+            if t == 0:
+                h1w(1, 0)
+                quant_w(1, 0)
+                quant_w(1, 1)
+            if t == 1:
+                spread(1, 0)
+                spread(1, 1)
+            if t == 2:
+                turn(1)
+                table(1)
         last = NSTEP - 1
-        squares(last)
+        square(last, 0)
+        norm_b(last - 2)
+        square(last, 1)
         reduce(last - 1)
-        norm(last - 1)
+        norm_a(last - 1)
         back(last - 2, 0)
         back(last - 2, 1)
         back(last - 1, 0)
         back(last - 1, 1)
         sumsq(last)
         evac(last - 2, 0)
+        norm_b(last - 1)
         evac(last - 2, 1)
         reduce(last)
+        norm_a(last)
         back(last, 0)
         back(last, 1)
-        evac(last - 1, 0)
         evac(last - 1, 1)
-        norm(last)
-        evac(last, 0)
+        evac(last - 1, 0)
+        norm_b(last)
         evac(last, 1)
+        evac(last, 0)

@@ -204,15 +204,10 @@ def tile_tttwrapper_pb_t_kernel(
             tps[hf] = tp
 
         def table(hf):
-            tabs[hf] = []
-            for k in range(3):
-                tab = const.tile([P, 512], BF16, name="tab%d%d" % (hf, k), tag="tab%d%d" % (hf, k))
-                src = tps[hf][:, min(k, 1) * 512 : (min(k, 1) + 1) * 512]
-                if k < 2:
-                    nc.scalar.copy(out=tab[:], in_=src)
-                else:
-                    nc.scalar.mul(out=tab[:], in_=src, mul=-1.0)
-                tabs[hf].append(tab)
+            tab = const.tile([P, 3, 512], BF16, name="tab%d" % hf, tag="tab%d" % hf)
+            nc.scalar.mul(out=tab[:, 0, :], in_=tps[hf][:, 512:1024], mul=-1.0)
+            nc.scalar.copy(out=tab[:, 1:3, :].rearrange("p k n -> p (k n)"), in_=tps[hf][:])
+            tabs[hf] = tab
 
         bcol = const.tile([P, 8], F32, name="bcol", tag="bcol")
         nc.scalar.copy(out=sc[:, 512:1024], in_=sc[:, 0:512])
@@ -274,22 +269,25 @@ def tile_tttwrapper_pb_t_kernel(
             acc[t] = pair
 
         def products(t, mid):
-            cs = tabs[(t // 4) % 2]
-            pa = work.tile([P, 1024], F32, name="pa", tag="pa", bufs=3)
-            pb = work.tile([P, 1024], F32, name="pb", tag="pb", bufs=3)
+            tab = tabs[(t // 4) % 2]
+            pa = work.tile([P, 2, 512], F32, name="pa", tag="pa", bufs=3)
+            pb = work.tile([P, 2, 512], F32, name="pb", tag="pb", bufs=3)
 
             def prod(out, e, k):
                 nc.vector.scalar_tensor_tensor(
-                    out=out, in0=acc[t][e][:], scalar=bias_col(t, e), in1=cs[k][:], op0=ALU.add, op1=ALU.mult
+                    out=out[:],
+                    in0=acc[t][e][:].unsqueeze(1).to_broadcast([P, 2, 512]),
+                    scalar=bias_col(t, e),
+                    in1=tab[:, k : k + 2, :],
+                    op0=ALU.add,
+                    op1=ALU.mult,
                 )
 
-            prod(pa[:, 0:512], 0, 0)
-            prod(pb[:, 0:512], 1, 2)
+            prod(pa, 0, 1)
             mid()
-            prod(pa[:, 512:1024], 0, 1)
-            prod(pb[:, 512:1024], 1, 0)
-            if t < TAIL_FROM:
-                o = work.tile([P, 1024], F32, name="o", tag="o", bufs=4)
+            prod(pb, 1, 0)
+            if t < NSTEP - 1:
+                o = work.tile([P, 2, 512], F32, name="o", tag="o", bufs=4)
                 nc.gpsimd.tensor_tensor(out=o[:], in0=pa[:], in1=pb[:], op=ALU.add)
                 rot[t] = (o,)
             else:
@@ -356,7 +354,7 @@ def tile_tttwrapper_pb_t_kernel(
                     for n in range(len(terms)):
                         nc.tensor.matmul(
                             out=bt[:, e * 256 + i2 * P : e * 256 + (i2 + 1) * P],
-                            lhsT=terms[n][:, e * 512 + i * P : e * 512 + (i + 1) * P],
+                            lhsT=terms[n][:, e, i * P : (i + 1) * P],
                             rhs=ident_f[:],
                             is_transpose=True,
                             start=(n == 0),
@@ -398,6 +396,16 @@ def tile_tttwrapper_pb_t_kernel(
             elif ip == 1:
                 nc.sync.dma_start(out=outv, in_=ot[:])
 
+        head = {}
+        for g in range(1, NG):
+            late = 1 if g == 1 else 0
+            for ip in range(2):
+                if g > 1:
+                    head[(4 * g - 5 + ip, 1)] = (g, ip)
+                head[(4 * g - 4 + ip + late, 2)] = (g, ip)
+                head[(4 * g - 4 + ip + late, 3)] = (g, ip)
+            head[(4 * g - 2, 4)] = (g,)
+        head[(1, 1)] = (1, 1)
         mx(0)
         for t in range(NSTEP):
             g, st = divmod(t, 4)
@@ -411,15 +419,15 @@ def tile_tttwrapper_pb_t_kernel(
                 norm_b(t - 3)
             if t >= 1:
                 square(t - 1, 1)
-            if more and st in (1, 2):
-                h2(nxt, st - 1)
+            if (t, 2) in head:
+                h2(*head[(t, 2)])
             if t >= 3:
                 evac(t - 3, 0)
                 back(t - 3, 1)
-            if more and st in (1, 2):
-                h3(nxt, st - 1)
-            if more and st in (0, 1) and t > 0:
-                h1w(nxt, st)
+            if (t, 3) in head:
+                h3(*head[(t, 3)])
+            if (t, 1) in head:
+                h1w(*head[(t, 1)])
             if t + 1 < NSTEP:
                 mx(t + 1)
             if t >= 3 and t < TAIL_FROM + 1:
@@ -433,8 +441,8 @@ def tile_tttwrapper_pb_t_kernel(
             products(t, mid)
             if t >= TAIL_FROM + 1:
                 evac(t - 3, 1)
-            if more and st == 2:
-                h4(nxt)
+            if (t, 4) in head:
+                h4(*head[(t, 4)])
             if t >= 1:
                 sumsq(t - 1)
             if t == 0:

@@ -17,6 +17,7 @@ AX = mybir.AxisListType
 
 P = 128
 NG = 8
+NIND = 64
 NSTEP = 32
 TAIL_FROM = 30
 
@@ -49,9 +50,9 @@ def tile_tttwrapper_pb_t_kernel(
         nc.sync.dma_start(
             out=hb[0][:], in_=hid[0:512, :].rearrange("(p i) k -> p (i k)", i=4)
         )
-        sc = const.tile([P, 1024], F32, name="sc", tag="sc")
+        sc4 = setup.tile([P, 4], F32, name="sc4", tag="sc4")
         nc.scalar.dma_start(
-            out=sc[:, 0:512], in_=hidden_states_scale.rearrange("a b k -> (a b k)").partition_broadcast(P)
+            out=sc4[:], in_=hidden_states_scale.rearrange("a b (p t) -> (a b p) t", t=4)
         )
         wraw = []
         for s, w in enumerate((wq_w, wu_w)):
@@ -70,16 +71,35 @@ def tile_tttwrapper_pb_t_kernel(
                 out=br[:].rearrange("p (q e) -> p q e", q=2), in_=b.rearrange("(q p e) -> p q e", q=2, e=2)
             )
             braw.append(br)
+        sc = const.tile([P, 1024], F32, name="sc", tag="sc")
         for g in range(1, NG):
             nc.sync.dma_start(
                 out=hb[g][:],
                 in_=hid[g * 512 : (g + 1) * 512, :].rearrange("(p i) k -> p (i k)", i=4),
             )
+            if g == 1:
+                nc.sync.dma_start(
+                    out=sc[:, 0:512], in_=hidden_states_scale.rearrange("a b k -> (a b k)").partition_broadcast(P)
+                )
 
+        warm = setup.tile([P, 512], BF16, name="warm", tag="warm")
+        nc.vector.memset(warm[:], 0.0)
+
+        def warm_up(n):
+            cold = ps_mx.tile([P, 512], F32, name="acc", tag="acc")
+            for i in range(n):
+                nc.tensor.matmul(out=cold[:], lhsT=warm[:, 0:P], rhs=warm[:], start=True, stop=True)
+
+        warm_up(4)
         ident_f = const.tile([P, P], F32, name="ident_f", tag="ident_f")
         make_identity(nc, ident_f[:])
         ident_b = const.tile([P, P], BF16, name="ident_b", tag="ident_b")
         make_identity(nc, ident_b[:])
+        ind = const.tile([P, NIND], F32, name="ind", tag="ind")
+        nc.vector.memset(ind[:], 0.0)
+        nc.vector.tensor_reduce(
+            out=ind[:, 0:4], in_=ident_f[:].rearrange("p (h j) -> p h j", h=4), axis=AX.X, op=ALU.add
+        )
         one = setup.tile([P, 1], F32, name="one", tag="one")
         nc.vector.memset(one[:], 1.0)
         eps = const.tile([P, 2], F32, name="eps", tag="eps")
@@ -99,13 +119,10 @@ def tile_tttwrapper_pb_t_kernel(
             wc.append(wc_s)
             ws.append(ws_s)
 
-        def interleave_w(s, hq, eng):
+        def interleave_w(s, hq):
             dst = wgs[s][:, hq * 1024 : (hq + 1) * 1024].rearrange("p (e x t) -> p e x t", e=2, t=4)
             src = wraw[s][:, :, hq * 256 : (hq + 1) * 256].rearrange("p t (x e) -> p e x t", e=2)
-            if eng == "v":
-                nc.vector.tensor_copy(out=dst, in_=src)
-            else:
-                nc.scalar.copy(out=dst, in_=src)
+            nc.scalar.copy(out=dst, in_=src)
 
         def quant_w(s, hq):
             cols = slice(hq * 256, (hq + 1) * 256)
@@ -120,14 +137,32 @@ def tile_tttwrapper_pb_t_kernel(
         hc = {}
         hs = {}
 
-        def h1(g, i):
-            if i == 0:
-                xb_g = work.tile([P, 2048], BF16, name="xb", tag="xb")
-                xb[g] = xb_g
+        xb0 = setup.tile([P, 2048], BF16, name="xb0", tag="xb0")
+        xg0 = setup.tile([P, 2048], BF16, name="xg0", tag="xg0", align_bytes=64)
+        xt0 = []
+
+        def first_widen(i):
+            nc.vector.tensor_copy(
+                out=xb0[:, i * 512 : (i + 1) * 512], in_=hb[0][:, i * 512 : (i + 1) * 512].bitcast(FP8)
+            )
+
+        def first_turn(ip):
+            xt = ps_bt.tile([P, 1024], BF16, name="xt0", tag="bt")
+            for i2 in range(2):
+                for t in range(4):
+                    i = ip * 2 + i2
+                    nc.tensor.transpose(
+                        xt[:, (t * 2 + i2) * P : (t * 2 + i2 + 1) * P],
+                        xb0[:, i * 512 + t : (i + 1) * 512 : 4],
+                        ident_b[:],
+                    )
+            xt0.append(xt)
+
+        def first_scale(ip):
             nc.vector.tensor_tensor(
-                out=xb[g][:, i * 512 : (i + 1) * 512],
-                in0=hb[g][:, i * 512 : (i + 1) * 512].bitcast(FP8),
-                in1=sc[:, 0:512],
+                out=xg0[:, ip * 1024 : (ip + 1) * 1024].rearrange("p (r t) -> p r t", t=4),
+                in0=xt0[ip][:].rearrange("p (t r) -> p r t", t=4),
+                in1=sc4[:].unsqueeze(1).to_broadcast([P, 256, 4]),
                 op=ALU.mult,
             )
 
@@ -146,10 +181,7 @@ def tile_tttwrapper_pb_t_kernel(
 
         def h2(g, ip):
             words = xb[g][:].bitcast(F32)
-            if g == 0 and ip == 1:
-                xt = ps_ss.tile([P, 512], F32, name="xt0", tag="ssp")
-            else:
-                xt = ps_xt.tile([P, 512], F32, name="xt", tag="xt")
+            xt = ps_xt.tile([P, 512], F32, name="xt", tag="xt")
             for i2 in range(2):
                 i = ip * 2 + i2
                 for u in range(2):
@@ -174,7 +206,9 @@ def tile_tttwrapper_pb_t_kernel(
         def h4(g):
             hc_g = work.tile([P, 512], U32, name="hc", tag="hc", align_bytes=64)
             hs_g = work.tile([P, 512], U8, name="hs", tag="hs", align_bytes=64)
-            nc.vector.quantize_mx(out=hc_g[:].bitcast(FP8X4), scales=hs_g[:], in_=xg[g][:])
+            nc.vector.quantize_mx(
+                out=hc_g[:].bitcast(FP8X4), scales=hs_g[:], in_=xg0[:] if g == 0 else xg[g][:]
+            )
             hc[g] = hc_g
             hs[g] = hs_g
 
@@ -210,31 +244,30 @@ def tile_tttwrapper_pb_t_kernel(
             tabs[hf] = tab
 
         bcol = const.tile([P, 8], F32, name="bcol", tag="bcol")
-        nc.scalar.copy(out=sc[:, 512:1024], in_=sc[:, 0:512])
         spread(0, 0)
         spread(0, 1)
-        h1(0, 0)
-        h1(0, 1)
-        h2(0, 0)
-        h1(0, 2)
-        h1(0, 3)
-        h3(0, 0)
-        h2(0, 1)
-        interleave_w(0, 0, "v")
-        interleave_w(0, 1, "v")
-        h3(0, 1)
-        quant_w(0, 0)
+        for i in range(4):
+            first_widen(i)
+        first_turn(0)
+        first_turn(1)
+        interleave_w(0, 0)
+        interleave_w(0, 1)
+        first_scale(0)
         for s in range(2):
             nc.vector.tensor_copy(
                 out=bcol[:].rearrange("p (e u q) -> p u e q", e=2, u=2)[:, s],
                 in_=braw[s][:].rearrange("p (q e) -> p e q", q=2),
             )
+        first_scale(1)
+        quant_w(0, 0)
         h4(0)
         quant_w(0, 1)
         turn(0)
+        warm_up(3)
         table(0)
-        interleave_w(1, 0, "s")
-        interleave_w(1, 1, "s")
+        nc.scalar.copy(out=sc[:, 512:1024], in_=sc[:, 0:512])
+        interleave_w(1, 0)
+        interleave_w(1, 1)
 
         acc = {}
         sq = {}
@@ -294,7 +327,7 @@ def tile_tttwrapper_pb_t_kernel(
                 rot[t] = (pa, pb)
 
         def square(t, e):
-            qt = work.tile([P, 512], F32, name="sq%d" % e, tag="sq%d" % e, bufs=2)
+            qt = work.tile([P, 512], F32, name="sq%d" % e, tag="sq%d" % e, bufs=3)
             nc.scalar.activation(
                 out=qt[:], in_=acc[t][e][:], func=ACT.Square, bias=bias_col(t, e), scale=1.0
             )
@@ -302,7 +335,7 @@ def tile_tttwrapper_pb_t_kernel(
 
         def sumsq(t):
             ssp = ps_ss.tile([P, 512], F32, name="ssp", tag="ssp")
-            for i in range(4):
+            for i in (2, 3):
                 for e in range(2):
                     nc.tensor.matmul(
                         out=ssp[:, i * P : (i + 1) * P],
@@ -314,13 +347,29 @@ def tile_tttwrapper_pb_t_kernel(
                     )
             ssps[t] = ssp
 
+        def sumsq_heads(t):
+            ssp = ssps[t]
+            for i in (0, 1):
+                for e in range(2):
+                    nc.tensor.matmul(
+                        out=ssp[:, i * NIND : (i + 1) * NIND],
+                        lhsT=sq[(t, e)][:, i * P : (i + 1) * P],
+                        rhs=ind[:],
+                        start=(e == 0),
+                        stop=(e == 1),
+                    )
+
         def reduce(t):
             ss = work.tile([P, 16], F32, name="ss", tag="ss", bufs=3)
             nc.vector.tensor_reduce(
-                out=ss[:],
-                in_=ssps[t][:].rearrange("p (i h j) -> p (i h) j", i=4, h=4),
+                out=ss[:, 8:16],
+                in_=ssps[t][:, 256:512].rearrange("p (i h j) -> p (i h) j", i=2, h=4),
                 axis=AX.X,
                 op=ALU.add,
+            )
+            nc.vector.tensor_copy(
+                out=ss[:, 0:8].rearrange("p (i h) -> p i h", i=2),
+                in_=ssps[t][:, 0 : 2 * NIND].rearrange("p (i n) -> p i n", i=2)[:, :, 0:4],
             )
             sss[t] = ss
 
@@ -372,7 +421,7 @@ def tile_tttwrapper_pb_t_kernel(
                 ot_t = work.tile([P, 4, 256], F32, name="ot", tag="ot", bufs=3)
                 ots[t] = ot_t
             ot = ots[t]
-            if ip == 1 and t >= TAIL_FROM - 2:
+            if ip == 1 and (t >= TAIL_FROM - 2 or t % 4 == 2):
                 nc.vector.tensor_tensor(
                     out=ot[:, 2:4, :].rearrange("p i (h j e) -> p (i h) j e", h=4, e=2),
                     in0=bts[(t, ip)][:].rearrange("p (e i h j) -> p (i h) j e", e=2, i=2, h=4),
@@ -411,6 +460,8 @@ def tile_tttwrapper_pb_t_kernel(
             g, st = divmod(t, 4)
             nxt = g + 1
             more = nxt < NG
+            if t >= 2:
+                sumsq_heads(t - 2)
             if t >= 3:
                 back(t - 3, 0)
             if t >= 1:
@@ -430,7 +481,8 @@ def tile_tttwrapper_pb_t_kernel(
                 h1w(*head[(t, 1)])
             if t + 1 < NSTEP:
                 mx(t + 1)
-            if t >= 3 and t < TAIL_FROM + 1:
+            vout = t >= TAIL_FROM + 1 or (t >= 3 and (t - 3) % 4 == 2)
+            if t >= 3 and not vout:
                 evac(t - 3, 1)
 
             def mid():
@@ -439,7 +491,7 @@ def tile_tttwrapper_pb_t_kernel(
                     norm_a(t - 2)
 
             products(t, mid)
-            if t >= TAIL_FROM + 1:
+            if vout:
                 evac(t - 3, 1)
             if (t, 4) in head:
                 h4(*head[(t, 4)])
@@ -459,6 +511,7 @@ def tile_tttwrapper_pb_t_kernel(
         square(last, 0)
         norm_b(last - 2)
         square(last, 1)
+        sumsq_heads(last - 1)
         reduce(last - 1)
         norm_a(last - 1)
         back(last - 2, 0)
@@ -469,6 +522,7 @@ def tile_tttwrapper_pb_t_kernel(
         evac(last - 2, 0)
         norm_b(last - 1)
         evac(last - 2, 1)
+        sumsq_heads(last)
         reduce(last)
         norm_a(last)
         back(last, 0)

@@ -17,7 +17,6 @@ AX = mybir.AxisListType
 
 P = 128
 NG = 8
-NIND = 64
 NSTEP = 32
 TAIL_FROM = 30
 
@@ -95,11 +94,6 @@ def tile_tttwrapper_pb_t_kernel(
         make_identity(nc, ident_f[:])
         ident_b = const.tile([P, P], BF16, name="ident_b", tag="ident_b")
         make_identity(nc, ident_b[:])
-        ind = const.tile([P, NIND], F32, name="ind", tag="ind")
-        nc.vector.memset(ind[:], 0.0)
-        nc.vector.tensor_reduce(
-            out=ind[:, 0:4], in_=ident_f[:].rearrange("p (h j) -> p h j", h=4), axis=AX.X, op=ALU.add
-        )
         one = setup.tile([P, 1], F32, name="one", tag="one")
         nc.vector.memset(one[:], 1.0)
         eps = const.tile([P, 2], F32, name="eps", tag="eps")
@@ -335,7 +329,7 @@ def tile_tttwrapper_pb_t_kernel(
 
         def sumsq(t):
             ssp = ps_ss.tile([P, 512], F32, name="ssp", tag="ssp")
-            for i in (2, 3):
+            for i in range(4):
                 for e in range(2):
                     nc.tensor.matmul(
                         out=ssp[:, i * P : (i + 1) * P],
@@ -347,29 +341,13 @@ def tile_tttwrapper_pb_t_kernel(
                     )
             ssps[t] = ssp
 
-        def sumsq_heads(t):
-            ssp = ssps[t]
-            for i in (0, 1):
-                for e in range(2):
-                    nc.tensor.matmul(
-                        out=ssp[:, i * NIND : (i + 1) * NIND],
-                        lhsT=sq[(t, e)][:, i * P : (i + 1) * P],
-                        rhs=ind[:],
-                        start=(e == 0),
-                        stop=(e == 1),
-                    )
-
         def reduce(t):
             ss = work.tile([P, 16], F32, name="ss", tag="ss", bufs=3)
             nc.vector.tensor_reduce(
-                out=ss[:, 8:16],
-                in_=ssps[t][:, 256:512].rearrange("p (i h j) -> p (i h) j", i=2, h=4),
+                out=ss[:],
+                in_=ssps[t][:].rearrange("p (i h j) -> p (i h) j", i=4, h=4),
                 axis=AX.X,
                 op=ALU.add,
-            )
-            nc.vector.tensor_copy(
-                out=ss[:, 0:8].rearrange("p (i h) -> p i h", i=2),
-                in_=ssps[t][:, 0 : 2 * NIND].rearrange("p (i n) -> p i n", i=2)[:, :, 0:4],
             )
             sss[t] = ss
 
@@ -421,11 +399,23 @@ def tile_tttwrapper_pb_t_kernel(
                 ot_t = work.tile([P, 4, 256], F32, name="ot", tag="ot", bufs=3)
                 ots[t] = ot_t
             ot = ots[t]
-            if ip == 1 and (t >= TAIL_FROM - 2 or t % 4 == 2):
+            if ip == 1 and t >= TAIL_FROM - 2:
                 nc.vector.tensor_tensor(
                     out=ot[:, 2:4, :].rearrange("p i (h j e) -> p (i h) j e", h=4, e=2),
                     in0=bts[(t, ip)][:].rearrange("p (e i h j) -> p (i h) j e", e=2, i=2, h=4),
                     in1=r[:, 8:16].unsqueeze(2).unsqueeze(3).to_broadcast([P, 8, 32, 2]),
+                    op=ALU.mult,
+                )
+            elif ip == 1 and t < TAIL_FROM - 4 and t % 4 == 1:
+                raw = work.tile([P, 512], F32, name="raw", tag="raw", bufs=2)
+                nc.scalar.copy(
+                    out=raw[:].rearrange("p (i j e) -> p i j e", i=8, e=2),
+                    in_=bts[(t, ip)][:].rearrange("p (e i h j) -> p (i h) j e", e=2, i=2, h=4),
+                )
+                nc.gpsimd.tensor_tensor(
+                    out=ot[:, 2:4, :].rearrange("p i (h d) -> p (i h) d", h=4),
+                    in0=raw[:].rearrange("p (i d) -> p i d", i=8),
+                    in1=r[:, 8:16].unsqueeze(2).to_broadcast([P, 8, 64]),
                     op=ALU.mult,
                 )
             else:
@@ -461,7 +451,7 @@ def tile_tttwrapper_pb_t_kernel(
             nxt = g + 1
             more = nxt < NG
             if t >= 2:
-                sumsq_heads(t - 2)
+                sumsq(t - 2)
             if t >= 3:
                 back(t - 3, 0)
             if t >= 1:
@@ -481,8 +471,7 @@ def tile_tttwrapper_pb_t_kernel(
                 h1w(*head[(t, 1)])
             if t + 1 < NSTEP:
                 mx(t + 1)
-            vout = t >= TAIL_FROM + 1 or (t >= 3 and (t - 3) % 4 == 2)
-            if t >= 3 and not vout:
+            if t >= 3 and t < TAIL_FROM + 1:
                 evac(t - 3, 1)
 
             def mid():
@@ -491,12 +480,10 @@ def tile_tttwrapper_pb_t_kernel(
                     norm_a(t - 2)
 
             products(t, mid)
-            if vout:
+            if t >= TAIL_FROM + 1:
                 evac(t - 3, 1)
             if (t, 4) in head:
                 h4(*head[(t, 4)])
-            if t >= 1:
-                sumsq(t - 1)
             if t == 0:
                 h1w(1, 0)
                 quant_w(1, 0)
@@ -511,7 +498,7 @@ def tile_tttwrapper_pb_t_kernel(
         square(last, 0)
         norm_b(last - 2)
         square(last, 1)
-        sumsq_heads(last - 1)
+        sumsq(last - 1)
         reduce(last - 1)
         norm_a(last - 1)
         back(last - 2, 0)
@@ -522,7 +509,6 @@ def tile_tttwrapper_pb_t_kernel(
         evac(last - 2, 0)
         norm_b(last - 1)
         evac(last - 2, 1)
-        sumsq_heads(last)
         reduce(last)
         norm_a(last)
         back(last, 0)

@@ -94,6 +94,12 @@ def tile_tttwrapper_pb_t_kernel(
         make_identity(nc, ident_f[:])
         ident_b = const.tile([P, P], BF16, name="ident_b", tag="ident_b")
         make_identity(nc, ident_b[:])
+        ident_r = const.tile([P, P], F32, name="ident_r", tag="ident_r")
+        for q in range(2):
+            nc.vector.tensor_copy(
+                out=ident_r[:].rearrange("p (h q j) -> p h q j", h=4, q=2)[:, :, q],
+                in_=ident_f[:].rearrange("p (h q j) -> p h q j", h=4, q=2)[:, :, 1 - q],
+            )
         one = setup.tile([P, 1], F32, name="one", tag="one")
         nc.vector.memset(one[:], 1.0)
         eps = const.tile([P, 2], F32, name="eps", tag="eps")
@@ -331,21 +337,22 @@ def tile_tttwrapper_pb_t_kernel(
             ssp = ps_ss.tile([P, 512], F32, name="ssp", tag="ssp")
             for i in range(4):
                 for e in range(2):
-                    nc.tensor.matmul(
-                        out=ssp[:, i * P : (i + 1) * P],
-                        lhsT=sq[(t, e)][:, i * P : (i + 1) * P],
-                        rhs=ident_f[:],
-                        is_transpose=True,
-                        start=(e == 0),
-                        stop=(e == 1),
-                    )
+                    for n, idn in enumerate((ident_f, ident_r) if t % 4 in (1,) else (ident_f,)):
+                        nc.tensor.matmul(
+                            out=ssp[:, i * P : (i + 1) * P],
+                            lhsT=sq[(t, e)][:, i * P : (i + 1) * P],
+                            rhs=idn[:],
+                            is_transpose=True,
+                            start=(e == 0 and n == 0),
+                            stop=(e == 1 and n == (1 if t % 4 in (1,) else 0)),
+                        )
             ssps[t] = ssp
 
         def reduce(t):
             ss = work.tile([P, 16], F32, name="ss", tag="ss", bufs=3)
             nc.vector.tensor_reduce(
                 out=ss[:],
-                in_=ssps[t][:].rearrange("p (i h j) -> p (i h) j", i=4, h=4),
+                in_=ssps[t][:].rearrange("p (i h j) -> p (i h) j", i=4, h=4)[:, :, 0 : 16 if t % 4 in (1,) else 32],
                 axis=AX.X,
                 op=ALU.add,
             )
@@ -404,18 +411,6 @@ def tile_tttwrapper_pb_t_kernel(
                     out=ot[:, 2:4, :].rearrange("p i (h j e) -> p (i h) j e", h=4, e=2),
                     in0=bts[(t, ip)][:].rearrange("p (e i h j) -> p (i h) j e", e=2, i=2, h=4),
                     in1=r[:, 8:16].unsqueeze(2).unsqueeze(3).to_broadcast([P, 8, 32, 2]),
-                    op=ALU.mult,
-                )
-            elif ip == 1 and t < TAIL_FROM - 4 and t % 4 == 1:
-                raw = work.tile([P, 512], F32, name="raw", tag="raw", bufs=2)
-                nc.scalar.copy(
-                    out=raw[:].rearrange("p (i j e) -> p i j e", i=8, e=2),
-                    in_=bts[(t, ip)][:].rearrange("p (e i h j) -> p (i h) j e", e=2, i=2, h=4),
-                )
-                nc.gpsimd.tensor_tensor(
-                    out=ot[:, 2:4, :].rearrange("p i (h d) -> p (i h) d", h=4),
-                    in0=raw[:].rearrange("p (i d) -> p i d", i=8),
-                    in1=r[:, 8:16].unsqueeze(2).to_broadcast([P, 8, 64]),
                     op=ALU.mult,
                 )
             else:

from contextlib import ExitStack

import concourse.mybir as mybir
from concourse.masks import make_identity

FLOPS = 2 * 4096 * 512 * 1024

F32 = mybir.dt.float32
BF16 = mybir.dt.bfloat16
U32 = mybir.dt.uint32
U8 = mybir.dt.uint8
FP8 = mybir.dt.float8_e4m3fn
FP8X4 = mybir.dt.float8_e4m3fn_x4
ALU = mybir.AluOpType
ACT = mybir.ActivationFunctionType
AX = mybir.AxisListType

P = 128
NG = 8
NSTEP = 32
TAIL_FROM = 30


def tile_tttwrapper_pb_t_kernel(
    tc, hidden_states_bytes, hidden_states_scale, freqs_cis, wq_w, wq_b, wu_w, wu_b, out_0, out_1
):
    nc = tc.nc
    with ExitStack() as ctx:
        const = ctx.enter_context(tc.tile_pool(name="const", bufs=1))
        setup = ctx.enter_context(tc.tile_pool(name="setup", bufs=1))
        work = ctx.enter_context(tc.tile_pool(name="work", bufs=2))
        ps_xt = ctx.enter_context(tc.psum_pool(name="ps_xt", bufs=1))
        ps_mx = ctx.enter_context(tc.psum_pool(name="ps_mx", bufs=4))
        ps_bt = ctx.enter_context(tc.psum_pool(name="ps_bt", bufs=2))
        ps_ss = ctx.enter_context(tc.psum_pool(name="ps_ss", bufs=1))

        hid = hidden_states_bytes.rearrange("b l k -> (b l) k")
        outs = [
            out_0.rearrange("b l h d -> (b l) (h d)"),
            out_1.rearrange("b l h d -> (b l) (h d)"),
        ]

        ctx.enter_context(tc.manual_schedule())

        hb = []
        for g in range(NG):
            hb_g = const.tile([P, 2048], U8, name="hbytes%d" % g, tag="hbytes%d" % g)
            hb.append(hb_g)
        nc.sync.dma_start(
            out=hb[0][:], in_=hid[0:512, :].rearrange("(p i) k -> p (i k)", i=4)
        )
        sc4 = setup.tile([P, 4], F32, name="sc4", tag="sc4")
        nc.scalar.dma_start(
            out=sc4[:], in_=hidden_states_scale.rearrange("a b (p t) -> (a b p) t", t=4)
        )
        wraw = []
        for s, w in enumerate((wq_w, wu_w)):
            wr = setup.tile([P, 4, 512], BF16, name="wraw%d" % s, tag="wraw%d" % s)
            nc.sync.dma_start(out=wr[:], in_=w.rearrange("(p t) n -> p t n", t=4))
            wraw.append(wr)
        fr = setup.tile([P, 512], BF16, name="fr", tag="fr")
        nc.scalar.dma_start(
            out=fr[:].rearrange("p (hf x) -> p hf x", hf=2),
            in_=freqs_cis.rearrange("(hf p i) j t -> p hf (i j t)", hf=2, p=P, i=4),
        )
        braw = []
        for s, b in enumerate((wq_b, wu_b)):
            br = setup.tile([P, 4], BF16, name="braw%d" % s, tag="braw%d" % s)
            nc.scalar.dma_start(
                out=br[:].rearrange("p (q e) -> p q e", q=2), in_=b.rearrange("(q p e) -> p q e", q=2, e=2)
            )
            braw.append(br)
        sc = const.tile([P, 1024], F32, name="sc", tag="sc")
        for g in range(1, NG):
            nc.sync.dma_start(
                out=hb[g][:],
                in_=hid[g * 512 : (g + 1) * 512, :].rearrange("(p i) k -> p (i k)", i=4),
            )
            if g == 1:
                nc.sync.dma_start(
                    out=sc[:, 0:512], in_=hidden_states_scale.rearrange("a b k -> (a b k)").partition_broadcast(P)
                )

        warm = setup.tile([P, 512], BF16, name="warm", tag="warm")
        nc.vector.memset(warm[:], 0.0)

        def warm_up(n):
            cold = ps_mx.tile([P, 512], F32, name="acc", tag="acc")
            for i in range(n):
                nc.tensor.matmul(out=cold[:], lhsT=warm[:, 0:P], rhs=warm[:], start=True, stop=True)

        warm_up(4)
        ident_f = const.tile([P, P], F32, name="ident_f", tag="ident_f")
        make_identity(nc, ident_f[:])
        ident_b = const.tile([P, P], BF16, name="ident_b", tag="ident_b")
        make_identity(nc, ident_b[:])
        ident_r = const.tile([P, P], F32, name="ident_r", tag="ident_r")
        for q in range(2):
            nc.vector.tensor_copy(
                out=ident_r[:].rearrange("p (h q j) -> p h q j", h=4, q=2)[:, :, q],
                in_=ident_f[:].rearrange("p (h q j) -> p h q j", h=4, q=2)[:, :, 1 - q],
            )
        one = setup.tile([P, 1], F32, name="one", tag="one")
        nc.vector.memset(one[:], 1.0)
        eps = const.tile([P, 2], F32, name="eps", tag="eps")
        nc.vector.memset(eps[:, 0:1], -1e-24)
        nc.vector.memset(eps[:, 1:2], 1e-24)
        junk = setup.tile([P, 1], F32, name="junk", tag="junk")
        nc.scalar.activation(out=junk[:], in_=one[:], func=ACT.Abs_reciprocal_sqrt)

        wc = []
        ws = []
        wgs = []
        for s in range(2):
            wg = setup.tile([P, 2048], BF16, name="wg%d" % s, tag="wg%d" % s, align_bytes=64)
            wgs.append(wg)
            wc_s = const.tile([P, 512], U32, name="wc%d" % s, tag="wc%d" % s, align_bytes=64)
            ws_s = const.tile([P, 512], U8, name="ws%d" % s, tag="ws%d" % s, align_bytes=64)
            wc.append(wc_s)
            ws.append(ws_s)

        def interleave_w(s, hq):
            dst = wgs[s][:, hq * 1024 : (hq + 1) * 1024].rearrange("p (e x t) -> p e x t", e=2, t=4)
            src = wraw[s][:, :, hq * 256 : (hq + 1) * 256].rearrange("p t (x e) -> p e x t", e=2)
            nc.scalar.copy(out=dst, in_=src)

        def quant_w(s, hq):
            cols = slice(hq * 256, (hq + 1) * 256)
            nc.vector.quantize_mx(
                out=wc[s][:, cols].bitcast(FP8X4),
                scales=ws[s][:, cols],
                in_=wgs[s][:, hq * 1024 : (hq + 1) * 1024],
            )

        xb = {}
        xg = {}
        hc = {}
        hs = {}

        xb0 = setup.tile([P, 2048], BF16, name="xb0", tag="xb0")
        xg0 = setup.tile([P, 2048], BF16, name="xg0", tag="xg0", align_bytes=64)
        xt0 = []

        def first_widen(i):
            nc.vector.tensor_copy(
                out=xb0[:, i * 512 : (i + 1) * 512], in_=hb[0][:, i * 512 : (i + 1) * 512].bitcast(FP8)
            )

        def first_turn(ip):
            xt = ps_bt.tile([P, 1024], BF16, name="xt0", tag="bt")
            for i2 in range(2):
                for t in range(4):
                    i = ip * 2 + i2
                    nc.tensor.transpose(
                        xt[:, (t * 2 + i2) * P : (t * 2 + i2 + 1) * P],
                        xb0[:, i * 512 + t : (i + 1) * 512 : 4],
                        ident_b[:],
                    )
            xt0.append(xt)

        def first_scale(ip):
            nc.vector.tensor_tensor(
                out=xg0[:, ip * 1024 : (ip + 1) * 1024].rearrange("p (r t) -> p r t", t=4),
                in0=xt0[ip][:].rearrange("p (t r) -> p r t", t=4),
                in1=sc4[:].unsqueeze(1).to_broadcast([P, 256, 4]),
                op=ALU.mult,
            )

        def h1w(g, ip):
            if ip == 0:
                xb_g = work.tile([P, 2048], BF16, name="xb", tag="xb")
                xb[g] = xb_g
            nc.vector.tensor_tensor(
                out=xb[g][:, ip * 1024 : (ip + 1) * 1024],
                in0=hb[g][:, ip * 1024 : (ip + 1) * 1024].bitcast(FP8),
                in1=sc[:],
                op=ALU.mult,
            )

        xts = {}

        def h2(g, ip):
            words = xb[g][:].bitcast(F32)
            xt = ps_xt.tile([P, 512], F32, name="xt", tag="xt")
            for i2 in range(2):
                i = ip * 2 + i2
                for u in range(2):
                    nc.tensor.transpose(
                        xt[:, (i2 * 2 + u) * P : (i2 * 2 + u + 1) * P],
                        words[:, i * 256 + u : (i + 1) * 256 : 2],
                        ident_f[:],
                    )
            xts[(g, ip)] = xt

        def h3(g, ip):
            if ip == 0:
                xg_g = work.tile([P, 2048], BF16, name="xg", tag="xg", align_bytes=64)
                xg[g] = xg_g
            nc.scalar.copy(
                out=xg[g][:].bitcast(F32)[:, ip * 512 : (ip + 1) * 512].rearrange(
                    "p (i r u) -> p i r u", i=2, u=2
                ),
                in_=xts[(g, ip)][:].rearrange("p (i u r) -> p i r u", i=2, u=2),
            )

        def h4(g):
            hc_g = work.tile([P, 512], U32, name="hc", tag="hc", align_bytes=64)
            hs_g = work.tile([P, 512], U8, name="hs", tag="hs", align_bytes=64)
            nc.vector.quantize_mx(
                out=hc_g[:].bitcast(FP8X4), scales=hs_g[:], in_=xg0[:] if g == 0 else xg[g][:]
            )
            hc[g] = hc_g
            hs[g] = hs_g

        exs = {}
        tabs = {}

        def spread(hf, k):
            ex = setup.tile([P, 512], BF16, name="ex%d%d" % (hf, k), tag="ex%d%d" % (hf, k))
            src = fr[:, hf * 256 : (hf + 1) * 256].rearrange("p (i j k) -> p i j k", i=4, k=2)[:, :, :, k]
            nc.scalar.copy(
                out=ex[:].rearrange("p (i h j) -> p i h j", i=4, h=4),
                in_=src.unsqueeze(2).to_broadcast([P, 4, 4, 32]),
            )
            exs[(hf, k)] = ex

        tps = {}

        def turn(hf):
            tp = ps_bt.tile([P, 1024], BF16, name="tp", tag="bt")
            for k in range(2):
                for i in range(4):
                    nc.tensor.transpose(
                        tp[:, k * 512 + i * P : k * 512 + (i + 1) * P],
                        exs[(hf, k)][:, i * P : (i + 1) * P],
                        ident_b[:],
                    )
            tps[hf] = tp

        def table(hf):
            tab = const.tile([P, 3, 512], BF16, name="tab%d" % hf, tag="tab%d" % hf)
            nc.scalar.mul(out=tab[:, 0, :], in_=tps[hf][:, 512:1024], mul=-1.0)
            nc.scalar.copy(out=tab[:, 1:3, :].rearrange("p k n -> p (k n)"), in_=tps[hf][:])
            tabs[hf] = tab

        bcol = const.tile([P, 8], F32, name="bcol", tag="bcol")
        spread(0, 0)
        spread(0, 1)
        for i in range(4):
            first_widen(i)
        first_turn(0)
        first_turn(1)
        interleave_w(0, 0)
        interleave_w(0, 1)
        first_scale(0)
        for s in range(2):
            nc.vector.tensor_copy(
                out=bcol[:].rearrange("p (e u q) -> p u e q", e=2, u=2)[:, s],
                in_=braw[s][:].rearrange("p (q e) -> p e q", q=2),
            )
        first_scale(1)
        quant_w(0, 0)
        h4(0)
        quant_w(0, 1)
        turn(0)
        warm_up(3)
        table(0)
        nc.scalar.copy(out=sc[:, 512:1024], in_=sc[:, 0:512])
        interleave_w(1, 0)
        interleave_w(1, 1)

        acc = {}
        sq = {}
        rot = {}
        rn = {}
        bts = {}
        ssps = {}
        sss = {}
        t1s = {}

        def bias_col(t, e):
            st = t % 4
            return bcol[:, e * 4 + st : e * 4 + st + 1]

        def mx(t):
            g, st = divmod(t, 4)
            s, hq = divmod(st, 2)
            pair = []
            for e in range(2):
                a = ps_mx.tile([P, 512], F32, name="acc", tag="acc")
                c0 = hq * 256 + e * P
                nc.tensor.matmul_mx(
                    out=a[:],
                    lhsT=wc[s][:, c0 : c0 + P].bitcast(FP8X4),
                    lhsT_scale=ws[s][:, c0 : c0 + P],
                    rhs=hc[g][:].bitcast(FP8X4),
                    rhs_scale=hs[g][:],
                    start=True,
                    stop=True,
                )
                pair.append(a)
            acc[t] = pair

        def products(t, mid):
            tab = tabs[(t // 4) % 2]
            pa = work.tile([P, 2, 512], F32, name="pa", tag="pa", bufs=3)
            pb = work.tile([P, 2, 512], F32, name="pb", tag="pb", bufs=3)

            def prod(out, e, k):
                nc.vector.scalar_tensor_tensor(
                    out=out[:],
                    in0=acc[t][e][:].unsqueeze(1).to_broadcast([P, 2, 512]),
                    scalar=bias_col(t, e),
                    in1=tab[:, k : k + 2, :],
                    op0=ALU.add,
                    op1=ALU.mult,
                )

            prod(pa, 0, 1)
            mid()
            prod(pb, 1, 0)
            if t < NSTEP - 1:
                o = work.tile([P, 2, 512], F32, name="o", tag="o", bufs=4)
                nc.gpsimd.tensor_tensor(out=o[:], in0=pa[:], in1=pb[:], op=ALU.add)
                rot[t] = (o,)
            else:
                rot[t] = (pa, pb)

        def square(t, e):
            qt = work.tile([P, 512], F32, name="sq%d" % e, tag="sq%d" % e, bufs=3)
            nc.scalar.activation(
                out=qt[:], in_=acc[t][e][:], func=ACT.Square, bias=bias_col(t, e), scale=1.0
            )
            sq[(t, e)] = qt

        def sumsq(t):
            ssp = ps_ss.tile([P, 512], F32, name="ssp", tag="ssp")
            for i in range(4):
                for e in range(2):
                    for n, idn in enumerate((ident_f, ident_r) if t % 4 in (1,) else (ident_f,)):
                        nc.tensor.matmul(
                            out=ssp[:, i * P : (i + 1) * P],
                            lhsT=sq[(t, e)][:, i * P : (i + 1) * P],
                            rhs=idn[:],
                            is_transpose=True,
                            start=(e == 0 and n == 0),
                            stop=(e == 1 and n == (1 if t % 4 in (1,) else 0)),
                        )
            ssps[t] = ssp

        def reduce(t):
            ss = work.tile([P, 16], F32, name="ss", tag="ss", bufs=3)
            nc.vector.tensor_reduce(
                out=ss[:],
                in_=ssps[t][:].rearrange("p (i h j) -> p (i h) j", i=4, h=4)[:, :, 0 : 16 if t % 4 in (1,) else 32],
                axis=AX.X,
                op=ALU.add,
            )
            sss[t] = ss

        def norm_a(t):
            t1 = work.tile([P, 16], F32, name="t1", tag="t1", bufs=3)
            nc.scalar.activation(
                out=t1[:],
                in_=sss[t][:],
                func=ACT.Relu,
                bias=eps[:, 0:1],
                scale=1.0,
            )
            t1s[t] = t1

        def norm_b(t):
            r = work.tile([P, 16], F32, name="r", tag="r", bufs=3)
            nc.scalar.activation(
                out=r[:], in_=t1s[t][:], func=ACT.Abs_reciprocal_sqrt, bias=eps[:, 1:2], scale=1.0
            )
            rn[t] = r

        def back(t, ip):
            if t >= NSTEP - 2:
                bt = ps_mx.tile([P, 512], F32, name="acc", tag="acc")
            else:
                bt = ps_bt.tile([P, 512], F32, name="bt", tag="bt")
            for e in range(2):
                for i2 in range(2):
                    i = ip * 2 + i2
                    terms = rot[t]
                    for n in range(len(terms)):
                        nc.tensor.matmul(
                            out=bt[:, e * 256 + i2 * P : e * 256 + (i2 + 1) * P],
                            lhsT=terms[n][:, e, i * P : (i + 1) * P],
                            rhs=ident_f[:],
                            is_transpose=True,
                            start=(n == 0),
                            stop=(n == len(terms) - 1),
                        )
            bts[(t, ip)] = bt

        ots = {}

        def evac(t, ip):
            g, st = divmod(t, 4)
            s, hq = divmod(st, 2)
            r = rn[t]
            if t not in ots:
                ot_t = work.tile([P, 4, 256], F32, name="ot", tag="ot", bufs=3)
                ots[t] = ot_t
            ot = ots[t]
            if ip == 1 and t >= TAIL_FROM - 2:
                nc.vector.tensor_tensor(
                    out=ot[:, 2:4, :].rearrange("p i (h j e) -> p (i h) j e", h=4, e=2),
                    in0=bts[(t, ip)][:].rearrange("p (e i h j) -> p (i h) j e", e=2, i=2, h=4),
                    in1=r[:, 8:16].unsqueeze(2).unsqueeze(3).to_broadcast([P, 8, 32, 2]),
                    op=ALU.mult,
                )
            else:
                v = bts[(t, ip)][:].rearrange("p (e i h j) -> p e i h j", e=2, i=2, h=4)
                for i2 in range(2):
                    i = ip * 2 + i2
                    for h in range(4):
                        nc.scalar.activation(
                            out=ot[:, i, h * 64 : (h + 1) * 64].rearrange("p (j e) -> p j e", e=2),
                            in_=v[:, :, i2, h, :].rearrange("p e j -> p j e"),
                            func=ACT.Copy,
                            scale=r[:, i * 4 + h : i * 4 + h + 1],
                        )
            outv = outs[s][g * 512 : (g + 1) * 512, hq * 256 : (hq + 1) * 256].rearrange("(p i) c -> p i c", i=4)
            if t >= TAIL_FROM:
                nc.sync.dma_start(out=outv[:, 2 * ip : 2 * ip + 2, :], in_=ot[:, 2 * ip : 2 * ip + 2, :])
            elif ip == 1:
                nc.sync.dma_start(out=outv, in_=ot[:])

        head = {}
        for g in range(1, NG):
            late = 1 if g == 1 else 0
            for ip in range(2):
                if g > 1:
                    head[(4 * g - 5 + ip, 1)] = (g, ip)
                head[(4 * g - 4 + ip + late, 2)] = (g, ip)
                head[(4 * g - 4 + ip + late, 3)] = (g, ip)
            head[(4 * g - 2, 4)] = (g,)
        head[(1, 1)] = (1, 1)
        mx(0)
        for t in range(NSTEP):
            g, st = divmod(t, 4)
            nxt = g + 1
            more = nxt < NG
            if t >= 2:
                sumsq(t - 2)
            if t >= 3:
                back(t - 3, 0)
            if t >= 1:
                square(t - 1, 0)
            if t >= 3:
                norm_b(t - 3)
            if t >= 1:
                square(t - 1, 1)
            if (t, 2) in head:
                h2(*head[(t, 2)])
            if t >= 3:
                evac(t - 3, 0)
                back(t - 3, 1)
            if (t, 3) in head:
                h3(*head[(t, 3)])
            if (t, 1) in head:
                h1w(*head[(t, 1)])
            if t + 1 < NSTEP:
                mx(t + 1)
            if t >= 3 and t < TAIL_FROM + 1:
                evac(t - 3, 1)

            def mid():
                if t >= 2:
                    reduce(t - 2)
                    norm_a(t - 2)

            products(t, mid)
            if t >= TAIL_FROM + 1:
                evac(t - 3, 1)
            if (t, 4) in head:
                h4(*head[(t, 4)])
            if t == 0:
                h1w(1, 0)
                quant_w(1, 0)
                quant_w(1, 1)
            if t == 1:
                spread(1, 0)
                spread(1, 1)
            if t == 2:
                turn(1)
                table(1)
        last = NSTEP - 1
        square(last, 0)
        norm_b(last - 2)
        square(last, 1)
        sumsq(last - 1)
        reduce(last - 1)
        norm_a(last - 1)
        back(last - 2, 0)
        back(last - 2, 1)
        back(last - 1, 0)
        back(last - 1, 1)
        sumsq(last)
        evac(last - 2, 0)
        norm_b(last - 1)
        evac(last - 2, 1)
        reduce(last)
        norm_a(last)
        back(last, 0)
        back(last, 1)
        evac(last - 1, 1)
        evac(last - 1, 0)
        norm_b(last)
        evac(last, 1)
        evac(last, 0)
